import numpy as np
import ml_dtypes


def mxq(x, axis, fmt="e4m3"):
    dtype, down = {"e4m3": (ml_dtypes.float8_e4m3fn, 7), "e5m2": (ml_dtypes.float8_e5m2, 14)}[fmt]
    v = np.moveaxis(np.asarray(x, np.float32).astype(ml_dtypes.bfloat16).astype(np.float64), axis, -1)
    blocks = v.reshape(v.shape[:-1] + (-1, 32))
    amax = np.abs(blocks).max(-1, keepdims=True)
    byte = np.maximum(np.where(amax > 0, np.frexp(amax)[1] - 1 + 127, 0) - down, 1)
    scale = np.exp2(byte - 127.0)
    codes = (blocks / scale).astype(np.float32).astype(dtype).astype(np.float64)
    return np.moveaxis((codes * scale).reshape(v.shape), -1, axis)


WIDE = False


def mx_kscale(k):
    if not WIDE:
        return np.ones(k)
    levels = np.array([10, -10, 5, -5, 0])
    a = np.random.permutation(np.resize(levels, k // 512 * 4)).reshape(k // 512, 4)
    idx = np.arange(k)
    return np.exp2(a[idx // 512, idx % 128 // 32])


BF16 = ml_dtypes.bfloat16


def bf(x):
    return np.asarray(x, np.float32).astype(BF16)


def f64(x):
    return np.asarray(x).astype(np.float64)


T, H, F = 512, 1024, 3584
BLK = 128


def silu(v):
    return v / (1.0 + np.exp(-v))


def _dequant(wq, scale_inv):
    N, K = wq.shape
    nb, kb = scale_inv.shape
    wb = wq.reshape(nb, N // nb, kb, K // kb) * scale_inv[:, None, :, None]
    return wb.reshape(N, K)


def setup_inputs():
    s, t = mx_kscale(H), mx_kscale(F)
    return {"hidden_states": bf(np.random.standard_normal((T, H)) * s),
            "w1_q": bf(np.random.standard_normal((F, H)) / s[None, :]),
            "w1_s": bf(0.03 * (0.5 + np.random.random((F // BLK, H // BLK)))),
            "w3_q": bf(np.random.standard_normal((F, H)) / s[None, :] * t[:, None]),
            "w3_s": bf(0.03 * (0.5 + np.random.random((F // BLK, H // BLK)))),
            "w2_q": bf(np.random.standard_normal((H, F)) / t[None, :]),
            "w2_s": bf(0.03 * (0.5 + np.random.random((H // BLK, F // BLK))))}


def reference(hidden_states, w1_q, w1_s, w3_q, w3_s, w2_q, w2_s):
    x = f64(hidden_states)
    w1 = _dequant(f64(w1_q), f64(w1_s))
    w3 = _dequant(f64(w3_q), f64(w3_s))
    w2 = _dequant(f64(w2_q), f64(w2_s))
    xq = mxq(x, 1, "e4m3")
    g = xq @ mxq(w1, 1, "e4m3").T
    u = xq @ mxq(w3, 1, "e4m3").T
    fused = silu(g) * u
    return mxq(fused, 1, "e4m3") @ mxq(w2, 1, "e4m3").T

@@ -1,0 +1,343 @@
+from contextlib import ExitStack
+
+import concourse.bass as bass
+import concourse.mybir as mybir
+import concourse.tile as tile
+from concourse.masks import make_identity
+
+F32 = mybir.dt.float32
+BF16 = mybir.dt.bfloat16
+U32 = mybir.dt.uint32
+U8 = mybir.dt.uint8
+FP8X4 = mybir.dt.float8_e4m3fn_x4
+ACT = mybir.ActivationFunctionType
+ALU = mybir.AluOpType
+
+T, H, F = 512, 1024, 3584
+P = 128
+FLOPS = 2 * T * H * F * 3
+
+LA = 2
+RAW_BUFS = 24
+SPAT = ((0,), (0, 3))
+SPAT_TAIL = ((0,),)
+
+
+def tile_blocksparsetop2mlphffp8_kernel(tc, hidden_states, w1_q, w1_s, w3_q, w3_s, w2_q, w2_s, out):
+    nc = tc.nc
+    with ExitStack() as ctx:
+        const = ctx.enter_context(tc.tile_pool(name="const", bufs=1))
+        rawp = ctx.enter_context(tc.tile_pool(name="rawp", bufs=RAW_BUFS))
+        grpp = ctx.enter_context(tc.tile_pool(name="grpp", bufs=8))
+        codp = ctx.enter_context(tc.tile_pool(name="codp", bufs=24))
+        sgp = ctx.enter_context(tc.tile_pool(name="sgp", bufs=3))
+        fgp = ctx.enter_context(tc.tile_pool(name="fgp", bufs=2))
+        w2cp = ctx.enter_context(tc.tile_pool(name="w2cp", bufs=4))
+        obp = ctx.enter_context(tc.tile_pool(name="obp", bufs=4))
+        psum = ctx.enter_context(tc.psum_pool(name="psum", bufs=4))
+        ctx.enter_context(tc.manual_schedule())
+
+        ident = const.tile([P, P], F32, name="ident")
+        make_identity(nc, ident[:])
+        perm = const.tile([P, P], F32, name="perm")
+        nc.vector.tensor_copy(
+            out=perm[:].rearrange("p (e m) -> p e m", e=2),
+            in_=ident[:].rearrange("p (m e) -> p e m", e=2),
+        )
+        warm_in = const.tile([P, 1], F32, name="warm_in")
+        warm_out = const.tile([P, 1], F32, name="warm_out")
+        nc.vector.memset(warm_in[:], 0.0)
+        nc.scalar.activation(out=warm_out[:], in_=warm_in[:], func=ACT.Silu)
+
+        sraw = const.tile([P, 672], BF16, name="sraw")
+        for i, sc in enumerate((w1_s, w3_s, w2_s)):
+            nc.scalar.dma_start(
+                out=sraw[:, 224 * i : 224 * (i + 1)],
+                in_=sc.rearrange("a b -> (a b)").partition_broadcast(P),
+            )
+        scb = const.tile([P, 352, 2], BF16, name="scb")
+        scf = const.tile([P, 336], F32, name="scf")
+        for half in range(2):
+            rows = slice(64 * half, 64 * half + 64)
+            src = sraw[rows, :].rearrange("p (m h) -> p m h", h=2)[:, :, half : half + 1]
+            nc.vector.tensor_copy(out=scf[rows, :].unsqueeze(2), in_=src)
+            nc.vector.tensor_copy(out=scb[rows, 0:336, :], in_=src.to_broadcast([64, 336, 2]))
+
+        xg = const.tile([P, 4096], BF16, name="xg", align_bytes=64)
+        xc = const.tile([P, 2, 512], U32, name="xc", align_bytes=64)
+        xs = const.tile([P, 2, 512], U8, name="xs", align_bytes=64)
+        fc = const.tile([P, 7, 512], U32, name="fc", align_bytes=64)
+        fs = const.tile([P, 7, 512], U8, name="fs", align_bytes=64)
+
+        runs = []
+        for c in range(7):
+            for w in (1, 3):
+                runs.append([((w, c, up, g), (w, c, up)) for up in range(2) for g in range(2)])
+        units2 = [(hh, c) for hh in range(2) for c in range(7)]
+        for j in range(7):
+            runs.append([((2,) + u + (q,), (2,) + u) for u in (units2[2 * j], units2[2 * j + 1]) for q in range(2)])
+        load_order = [("x", 0), ("x", 1)]
+        for r in runs:
+            for bk, ru in r:
+                if ru not in load_order:
+                    load_order.append(ru)
+
+        raw_t = {}
+        bank_t = {}
+        grp_t = {}
+        cod_t = {}
+        w2c_t = {}
+        state = {"loaded": 0, "used": 0}
+
+        def nm(bk):
+            return ("%s_" * len(bk)) % tuple(bk)
+
+        def load_upto(n):
+            while state["loaded"] < min(n, len(load_order)):
+                u = load_order[state["loaded"]]
+                t = rawp.tile([P, 2048], BF16, name="raw_" + nm(u), tag="raw")
+                raw_t[u] = t
+                if u[0] == "x":
+                    src = hidden_states[256 * u[1] : 256 * u[1] + 256, :].rearrange("(b p) k -> p b k", p=P)
+                    dst = t[:].rearrange("p (b k) -> p b k", b=2)
+                elif u[0] == 2:
+                    hh, c = u[1], u[2]
+                    src = w2_q[512 * hh : 512 * hh + 512, 512 * c : 512 * c + 512].rearrange("(b p) f -> p b f", p=P)
+                    dst = t[:].rearrange("p (b f) -> p b f", b=4)
+                else:
+                    wq = w1_q if u[0] == 1 else w3_q
+                    r0 = 512 * u[1] + 256 * u[2]
+                    src = wq[r0 : r0 + 256, :].rearrange("(b p) k -> p b k", p=P)
+                    dst = t[:].rearrange("p (b k) -> p b k", b=2)
+                nc.sync.dma_start(out=dst, in_=src)
+                state["loaded"] += 1
+
+        def t_bank(bk, ru):
+            bank = psum.tile([P, 512], F32, name="T_" + nm(bk), tag="T")
+            bank_t[bk] = bank
+            rf = raw_t[ru][:].bitcast(F32)
+            for u in range(2):
+                for b in range(2):
+                    if bk[0] == 2:
+                        col = (2 * bk[3] + b) * 256 + 128 * u
+                        mat = ident
+                    else:
+                        col = b * 512 + 256 * bk[3] + 128 * u
+                        mat = perm
+                    nc.tensor.transpose(bank[:, (2 * u + b) * P : (2 * u + b + 1) * P], rf[:, col : col + P], mat[:])
+
+        def t_run(r):
+            for bk, ru in runs[r]:
+                t_bank(bk, ru)
+            state["used"] += 2
+            load_upto(state["used"] + RAW_BUFS)
+
+        def is_s(r, i):
+            pat = SPAT[r % len(SPAT)] if r < 14 else SPAT_TAIL[r % len(SPAT_TAIL)]
+            return i in pat
+
+        def sc_index(bk, b, u):
+            if bk[0] == 2:
+                hh, c, q = bk[1], bk[2], bk[3]
+                return 224 + (4 * hh + 2 * q + b) * 14 + 2 * c + u
+            base = 0 if bk[0] == 1 else 112
+            return base + (4 * bk[1] + 2 * bk[2] + b) * 4 + 2 * bk[3] + u
+
+        def ex(r, i):
+            bk, ru = runs[r][i]
+            bank = bank_t[bk]
+            grp = grpp.tile([P, 1024], BF16, name="grp_" + nm(bk), tag="grp", align_bytes=64)
+            grp_t[bk] = grp
+            bbf = bank[:].bitcast(BF16)
+            if bk[0] == 2:
+                gview = grp[:].rearrange("p (b h m u e) -> p b h m u e", b=2, h=2, m=64, u=2, e=2)
+            else:
+                gview = grp[:].rearrange("p (h b m u e) -> p b h m u e", b=2, h=2, m=64, u=2, e=2)
+            if is_s(r, i):
+                for b in range(2):
+                    for u in range(2):
+                        k = sc_index(bk, b, u)
+                        nc.scalar.activation(
+                            out=gview[:, b, :, :, u, :],
+                            in_=bbf[:, (2 * u + b) * 256 : (2 * u + b + 1) * 256].rearrange(
+                                "p (h m e) -> p h m e", h=2, m=64, e=2
+                            ),
+                            func=ACT.Copy,
+                            scale=scf[:, k : k + 1],
+                        )
+            else:
+                k0 = sc_index(bk, 0, 0)
+                step = sc_index(bk, 1, 0) - k0
+                tab = scb[:, k0 : k0 + 2 * step, :].rearrange("p (b j) e -> p b (j e)", b=2)[:, :, 0:4]
+                if bk[0] == 2:
+                    dst = grp[:].rearrange("p (n u e) -> p n u e", u=2, e=2)
+                else:
+                    dst = grp[:].rearrange("p (h b x) -> p b h x", h=2, b=2)
+                nc.vector.tensor_tensor(
+                    out=dst,
+                    in0=bbf.rearrange("p (u n e) -> p n u e", u=2, e=2),
+                    in1=tab.unsqueeze(2).to_broadcast([P, 2, P, 4]),
+                    op=ALU.mult,
+                )
+
+        def q(r, i):
+            bk, ru = runs[r][i]
+            if bk[0] == 2:
+                key = bk[1:3]
+                if key not in w2c_t:
+                    wc = w2cp.tile([P, 512], U32, name="w2c_" + nm(key), tag="w2c", align_bytes=64)
+                    ws = w2cp.tile([P, 512], U8, name="w2s_" + nm(key), tag="w2s", align_bytes=64)
+                    w2c_t[key] = (wc, ws)
+                wc, ws = w2c_t[key]
+                sl = slice(256 * bk[3], 256 * bk[3] + 256)
+                nc.vector.quantize_mx(out=wc[:, sl].bitcast(FP8X4), scales=ws[:, sl], in_=grp_t[bk][:])
+            else:
+                cd = codp.tile([P, 256], U32, name="cod_" + nm(bk), tag="cod", align_bytes=64)
+                cs = codp.tile([P, 256], U8, name="cos_" + nm(bk), tag="cos", align_bytes=64)
+                cod_t[bk] = (cd, cs)
+                nc.vector.quantize_mx(out=cd[:].bitcast(FP8X4), scales=cs[:], in_=grp_t[bk][:])
+
+        load_upto(RAW_BUFS)
+        xgf = xg[:].bitcast(F32).rearrange("p (g t r u) -> p t g r u", g=2, t=4, r=P, u=2)
+        xbanks = []
+        for t in range(4):
+            bank = psum.tile([P, 512], F32, name="TX_%d" % t, tag="T")
+            xbanks.append(bank)
+            rf = raw_t[("x", t // 2)][:].bitcast(F32)
+            for u in range(2):
+                for g in range(2):
+                    col = (t % 2) * 512 + 256 * g + 128 * u
+                    nc.tensor.transpose(bank[:, (2 * u + g) * P : (2 * u + g + 1) * P], rf[:, col : col + P], ident[:])
+        for t in range(4):
+            src = xbanks[t][:].rearrange("p (u g r) -> p g r u", u=2, g=2, r=P)
+            if t % 2:
+                nc.scalar.copy(out=xgf[:, t], in_=src)
+            else:
+                nc.vector.tensor_copy(out=xgf[:, t], in_=src)
+        for g in range(2):
+            nc.vector.quantize_mx(
+                out=xc[:, g, :].bitcast(FP8X4), scales=xs[:, g, :], in_=xg[:, 2048 * g : 2048 * (g + 1)]
+            )
+        state["used"] = 2
+
+        def emit_exits(r):
+            for i in range(4):
+                if is_s(r, i) and i < 2:
+                    ex(r, i)
+            for i in range(4):
+                if not is_s(r, i):
+                    ex(r, i)
+
+        def late_s(r):
+            for i in range(4):
+                if is_s(r, i) and i >= 2:
+                    ex(r, i)
+
+        for r in range(LA):
+            t_run(r)
+            emit_exits(r)
+            late_s(r)
+            for i in range(4):
+                q(r, i)
+
+        gu_t = {}
+        sg_t = {}
+        fg_t = {}
+
+        def mm1(kind, w, c, tb):
+            bank = psum.tile([P, 512], F32, name="%s_%d_%d" % (kind, c, tb), tag="GU")
+            gu_t[(kind, c, tb)] = bank
+            for tau in range(4):
+                up, e = tau // 2, tau % 2
+                for g in range(2):
+                    cd, cs = cod_t[(w, c, up, g)]
+                    nc.tensor.matmul_mx(
+                        out=bank[:, tau * P : (tau + 1) * P],
+                        lhsT=cd[:, e * P : (e + 1) * P].bitcast(FP8X4),
+                        lhsT_scale=cs[:, e * P : (e + 1) * P],
+                        rhs=xc[:, g, tb * P : (tb + 1) * P].bitcast(FP8X4),
+                        rhs_scale=xs[:, g, tb * P : (tb + 1) * P],
+                        start=(g == 0),
+                        stop=(g == 1),
+                    )
+
+        def silu(c, tb):
+            sg = sgp.tile([P, P, 4], F32, name="sg_%d_%d" % (c, tb), tag="sg")
+            sg_t[(c, tb)] = sg
+            nc.scalar.activation(
+                out=sg[:], in_=gu_t[("g", c, tb)][:].rearrange("p (t r) -> p r t", t=4), func=ACT.Silu
+            )
+
+        def gate(c, tb):
+            if c not in fg_t:
+                fg_t[c] = fgp.tile([P, 4, P, 4], BF16, name="fg_%d" % c, tag="fg", align_bytes=64)
+            nc.vector.tensor_tensor(
+                out=fg_t[c][:, tb, :, :],
+                in0=gu_t[("u", c, tb)][:].rearrange("p (t r) -> p r t", t=4),
+                in1=sg_t[(c, tb)][:],
+                op=ALU.mult,
+            )
+
+        def qf(c):
+            nc.vector.quantize_mx(
+                out=fc[:, c, :].bitcast(FP8X4), scales=fs[:, c, :], in_=fg_t[c][:].rearrange("p a r t -> p (a r t)")
+            )
+
+        lag = []
+        acc_t = {}
+        for k in range(21):
+            r = k + LA
+            if r < 21:
+                t_run(r)
+                emit_exits(r)
+            for item in lag:
+                gate(item[0], item[1])
+                if item[2]:
+                    qf(item[0])
+            lag = []
+            if k < 14:
+                c, h = k // 2, k % 2
+                a, b = 2 * h, 2 * h + 1
+                for tb in (a, b):
+                    mm1("g", 1, c, tb)
+                    mm1("u", 3, c, tb)
+                silu(c, a)
+                if r < 21:
+                    late_s(r)
+                silu(c, b)
+                if r < 21:
+                    for i in range(4):
+                        q(r, i)
+                gate(c, a)
+                lag.append((c, b, h == 1))
+            else:
+                j = k - 14
+                for u2 in (units2[2 * j], units2[2 * j + 1]):
+                    hh, c = u2
+                    wc, ws = w2c_t[u2]
+                    for tb in range(4):
+                        if c == 0:
+                            acc_t[(hh, tb)] = psum.tile([P, 512], F32, name="acc_%d_%d" % (hh, tb), tag="GU")
+                        acc = acc_t[(hh, tb)]
+                        nc.tensor.matmul_mx(
+                            out=acc[:],
+                            lhsT=fc[:, c, tb * P : (tb + 1) * P].bitcast(FP8X4),
+                            lhsT_scale=fs[:, c, tb * P : (tb + 1) * P],
+                            rhs=wc[:].bitcast(FP8X4),
+                            rhs_scale=ws[:],
+                            start=(c == 0),
+                            stop=(c == 6),
+                        )
+                        if c == 6:
+                            ob = obp.tile([P, 512], F32, name="ob_%d_%d" % (hh, tb), tag="ob")
+                            if tb % 2 == 0:
+                                nc.scalar.copy(out=ob[:], in_=acc[:])
+                            else:
+                                nc.vector.tensor_copy(out=ob[:], in_=acc[:])
+                            nc.sync.dma_start(
+                                out=out[tb * P : (tb + 1) * P, hh * 512 : (hh + 1) * 512], in_=ob[:]
+                            )
+                if r < 21:
+                    late_s(r)
+                    for i in range(4):
+                        q(r, i)

@@ -1,8 +1,6 @@
 from contextlib import ExitStack
 
-import concourse.bass as bass
 import concourse.mybir as mybir
-import concourse.tile as tile
 from concourse.masks import make_identity
 
 F32 = mybir.dt.float32
@@ -17,10 +15,8 @@ T, H, F = 512, 1024, 3584
 P = 128
 FLOPS = 2 * T * H * F * 3
 
-LA = 2
-RAW_BUFS = 24
-SPAT = ((0,), (0, 3))
-SPAT_TAIL = ((0,),)
+LA = 3
+RAW_BUFS = 18
 
 
 def tile_blocksparsetop2mlphffp8_kernel(tc, hidden_states, w1_q, w1_s, w3_q, w3_s, w2_q, w2_s, out):
@@ -28,22 +24,16 @@ def tile_blocksparsetop2mlphffp8_kernel(tc, hidden_states, w1_q, w1_s, w3_q, w3_
     with ExitStack() as ctx:
         const = ctx.enter_context(tc.tile_pool(name="const", bufs=1))
         rawp = ctx.enter_context(tc.tile_pool(name="rawp", bufs=RAW_BUFS))
-        grpp = ctx.enter_context(tc.tile_pool(name="grpp", bufs=8))
-        codp = ctx.enter_context(tc.tile_pool(name="codp", bufs=24))
+        grpp = ctx.enter_context(tc.tile_pool(name="grpp", bufs=4))
+        codp = ctx.enter_context(tc.tile_pool(name="codp", bufs=7))
         sgp = ctx.enter_context(tc.tile_pool(name="sgp", bufs=3))
         fgp = ctx.enter_context(tc.tile_pool(name="fgp", bufs=2))
-        w2cp = ctx.enter_context(tc.tile_pool(name="w2cp", bufs=4))
         obp = ctx.enter_context(tc.tile_pool(name="obp", bufs=4))
         psum = ctx.enter_context(tc.psum_pool(name="psum", bufs=4))
         ctx.enter_context(tc.manual_schedule())
 
         ident = const.tile([P, P], F32, name="ident")
         make_identity(nc, ident[:])
-        perm = const.tile([P, P], F32, name="perm")
-        nc.vector.tensor_copy(
-            out=perm[:].rearrange("p (e m) -> p e m", e=2),
-            in_=ident[:].rearrange("p (m e) -> p e m", e=2),
-        )
         warm_in = const.tile([P, 1], F32, name="warm_in")
         warm_out = const.tile([P, 1], F32, name="warm_out")
         nc.vector.memset(warm_in[:], 0.0)
@@ -55,13 +45,30 @@ def tile_blocksparsetop2mlphffp8_kernel(tc, hidden_states, w1_q, w1_s, w3_q, w3_
                 out=sraw[:, 224 * i : 224 * (i + 1)],
                 in_=sc.rearrange("a b -> (a b)").partition_broadcast(P),
             )
-        scb = const.tile([P, 352, 2], BF16, name="scb")
-        scf = const.tile([P, 336], F32, name="scf")
+        scb = const.tile([P, 336, 2], BF16, name="scb")
         for half in range(2):
             rows = slice(64 * half, 64 * half + 64)
             src = sraw[rows, :].rearrange("p (m h) -> p m h", h=2)[:, :, half : half + 1]
-            nc.vector.tensor_copy(out=scf[rows, :].unsqueeze(2), in_=src)
-            nc.vector.tensor_copy(out=scb[rows, 0:336, :], in_=src.to_broadcast([64, 336, 2]))
+            nc.vector.tensor_copy(out=scb[rows, :, :], in_=src.to_broadcast([64, 336, 2]))
+        tabs = {}
+        for i, w in enumerate((1, 3)):
+            tab = const.tile([P, 112, 4], BF16, name="tab%d" % w)
+            tabs[w] = tab
+            for g in range(2):
+                for e in range(2):
+                    nc.vector.tensor_copy(
+                        out=tab[:].rearrange("p (a g h r) x -> p a g h r x", g=2, h=2, r=2)[:, :, g, e, :, :],
+                        in_=scb[:, 112 * i : 112 * (i + 1), :].rearrange(
+                            "p (a r g u) e -> p a r g (u e)", r=2, g=2, u=2
+                        )[:, :, :, g, :],
+                    )
+        tab2 = const.tile([P, 56, 4], BF16, name="tab2")
+        tabs[2] = tab2
+        for hh in range(2):
+            nc.vector.tensor_copy(
+                out=tab2[:, 28 * hh : 28 * (hh + 1), :].rearrange("p (c b) x -> p c b x", b=4),
+                in_=scb[:, 224:336, :].rearrange("p (hh b c u) e -> p hh c b (u e)", hh=2, b=4, c=7, u=2)[:, hh],
+            )
 
         xg = const.tile([P, 4096], BF16, name="xg", align_bytes=64)
         xc = const.tile([P, 2, 512], U32, name="xc", align_bytes=64)
@@ -86,7 +93,6 @@ def tile_blocksparsetop2mlphffp8_kernel(tc, hidden_states, w1_q, w1_s, w3_q, w3_
         bank_t = {}
         grp_t = {}
         cod_t = {}
-        w2c_t = {}
         state = {"loaded": 0, "used": 0}
 
         def nm(bk):
@@ -107,95 +113,57 @@ def tile_blocksparsetop2mlphffp8_kernel(tc, hidden_states, w1_q, w1_s, w3_q, w3_
                 else:
                     wq = w1_q if u[0] == 1 else w3_q
                     r0 = 512 * u[1] + 256 * u[2]
-                    src = wq[r0 : r0 + 256, :].rearrange("(b p) k -> p b k", p=P)
-                    dst = t[:].rearrange("p (b k) -> p b k", b=2)
+                    src = wq[r0 : r0 + 256, :].rearrange("(p e) k -> p (e k)", e=2)
+                    dst = t[:]
                 nc.sync.dma_start(out=dst, in_=src)
                 state["loaded"] += 1
 
-        def t_bank(bk, ru):
-            bank = psum.tile([P, 512], F32, name="T_" + nm(bk), tag="T")
-            bank_t[bk] = bank
-            rf = raw_t[ru][:].bitcast(F32)
-            for u in range(2):
-                for b in range(2):
-                    if bk[0] == 2:
-                        col = (2 * bk[3] + b) * 256 + 128 * u
-                        mat = ident
-                    else:
-                        col = b * 512 + 256 * bk[3] + 128 * u
-                        mat = perm
-                    nc.tensor.transpose(bank[:, (2 * u + b) * P : (2 * u + b + 1) * P], rf[:, col : col + P], mat[:])
-
         def t_run(r):
             for bk, ru in runs[r]:
-                t_bank(bk, ru)
+                bank = psum.tile([P, 512], F32, name="T_" + nm(bk), tag="T")
+                bank_t[bk] = bank
+                rf = raw_t[ru][:].bitcast(F32)
+                for u in range(2):
+                    for b in range(2):
+                        if bk[0] == 2:
+                            col = (2 * bk[3] + b) * 256 + 128 * u
+                        else:
+                            col = b * 512 + 256 * bk[3] + 128 * u
+                        nc.tensor.transpose(
+                            bank[:, (2 * u + b) * P : (2 * u + b + 1) * P], rf[:, col : col + P], ident[:]
+                        )
             state["used"] += 2
             load_upto(state["used"] + RAW_BUFS)
 
-        def is_s(r, i):
-            pat = SPAT[r % len(SPAT)] if r < 14 else SPAT_TAIL[r % len(SPAT_TAIL)]
-            return i in pat
-
-        def sc_index(bk, b, u):
-            if bk[0] == 2:
-                hh, c, q = bk[1], bk[2], bk[3]
-                return 224 + (4 * hh + 2 * q + b) * 14 + 2 * c + u
-            base = 0 if bk[0] == 1 else 112
-            return base + (4 * bk[1] + 2 * bk[2] + b) * 4 + 2 * bk[3] + u
-
-        def ex(r, i):
-            bk, ru = runs[r][i]
-            bank = bank_t[bk]
-            grp = grpp.tile([P, 1024], BF16, name="grp_" + nm(bk), tag="grp", align_bytes=64)
-            grp_t[bk] = grp
-            bbf = bank[:].bitcast(BF16)
-            if bk[0] == 2:
-                gview = grp[:].rearrange("p (b h m u e) -> p b h m u e", b=2, h=2, m=64, u=2, e=2)
-            else:
-                gview = grp[:].rearrange("p (h b m u e) -> p b h m u e", b=2, h=2, m=64, u=2, e=2)
-            if is_s(r, i):
-                for b in range(2):
-                    for u in range(2):
-                        k = sc_index(bk, b, u)
-                        nc.scalar.activation(
-                            out=gview[:, b, :, :, u, :],
-                            in_=bbf[:, (2 * u + b) * 256 : (2 * u + b + 1) * 256].rearrange(
-                                "p (h m e) -> p h m e", h=2, m=64, e=2
-                            ),
-                            func=ACT.Copy,
-                            scale=scf[:, k : k + 1],
-                        )
-            else:
-                k0 = sc_index(bk, 0, 0)
-                step = sc_index(bk, 1, 0) - k0
-                tab = scb[:, k0 : k0 + 2 * step, :].rearrange("p (b j) e -> p b (j e)", b=2)[:, :, 0:4]
-                if bk[0] == 2:
-                    dst = grp[:].rearrange("p (n u e) -> p n u e", u=2, e=2)
-                else:
-                    dst = grp[:].rearrange("p (h b x) -> p b h x", h=2, b=2)
-                nc.vector.tensor_tensor(
-                    out=dst,
-                    in0=bbf.rearrange("p (u n e) -> p n u e", u=2, e=2),
-                    in1=tab.unsqueeze(2).to_broadcast([P, 2, P, 4]),
-                    op=ALU.mult,
+        def s_copies(r):
+            grp = grpp.tile([P, 4096], BF16, name="grp_%d" % r, tag="grp", align_bytes=64)
+            grp_t[r] = grp
+            gf = grp[:].bitcast(F32)
+            for i in range(4):
+                bk, ru = runs[r][i]
+                nc.scalar.copy(
+                    out=gf[:, 512 * i : 512 * (i + 1)].rearrange("p (n u) -> p n u", u=2),
+                    in_=bank_t[bk][:].rearrange("p (u n) -> p n u", u=2),
                 )
 
-        def q(r, i):
-            bk, ru = runs[r][i]
-            if bk[0] == 2:
-                key = bk[1:3]
-                if key not in w2c_t:
-                    wc = w2cp.tile([P, 512], U32, name="w2c_" + nm(key), tag="w2c", align_bytes=64)
-                    ws = w2cp.tile([P, 512], U8, name="w2s_" + nm(key), tag="w2s", align_bytes=64)
-                    w2c_t[key] = (wc, ws)
-                wc, ws = w2c_t[key]
-                sl = slice(256 * bk[3], 256 * bk[3] + 256)
-                nc.vector.quantize_mx(out=wc[:, sl].bitcast(FP8X4), scales=ws[:, sl], in_=grp_t[bk][:])
+        def v_scale(r):
+            grp = grp_t[r]
+            kind = runs[r][0][0][0]
+            if kind == 2:
+                j = r - 14
+                view = grp[:].rearrange("p (j n x) -> p j n x", n=128, x=4)
+                tab = tabs[2][:, 8 * j : 8 * (j + 1), :].unsqueeze(2).to_broadcast([P, 8, 128, 4])
             else:
-                cd = codp.tile([P, 256], U32, name="cod_" + nm(bk), tag="cod", align_bytes=64)
-                cs = codp.tile([P, 256], U8, name="cos_" + nm(bk), tag="cos", align_bytes=64)
-                cod_t[bk] = (cd, cs)
-                nc.vector.quantize_mx(out=cd[:].bitcast(FP8X4), scales=cs[:], in_=grp_t[bk][:])
+                c = runs[r][0][0][1]
+                view = grp[:].rearrange("p (j n x) -> p j n x", n=64, x=4)
+                tab = tabs[kind][:, 16 * c : 16 * (c + 1), :].unsqueeze(2).to_broadcast([P, 16, 64, 4])
+            nc.vector.tensor_tensor(out=view, in0=view, in1=tab, op=ALU.mult)
+
+        def v_quant(r):
+            cd = codp.tile([P, 1024], U32, name="cod_%d" % r, tag="cod", align_bytes=64)
+            cs = codp.tile([P, 1024], U8, name="cos_%d" % r, tag="cos", align_bytes=64)
+            cod_t[r] = (cd, cs)
+            nc.vector.quantize_mx(out=cd[:].bitcast(FP8X4), scales=cs[:], in_=grp_t[r][:])
 
         load_upto(RAW_BUFS)
         xgf = xg[:].bitcast(F32).rearrange("p (g t r u) -> p t g r u", g=2, t=4, r=P, u=2)
@@ -220,25 +188,11 @@ def tile_blocksparsetop2mlphffp8_kernel(tc, hidden_states, w1_q, w1_s, w3_q, w3_
             )
         state["used"] = 2
 
-        def emit_exits(r):
-            for i in range(4):
-                if is_s(r, i) and i < 2:
-                    ex(r, i)
-            for i in range(4):
-                if not is_s(r, i):
-                    ex(r, i)
-
-        def late_s(r):
-            for i in range(4):
-                if is_s(r, i) and i >= 2:
-                    ex(r, i)
-
         for r in range(LA):
             t_run(r)
-            emit_exits(r)
-            late_s(r)
-            for i in range(4):
-                q(r, i)
+            s_copies(r)
+            v_scale(r)
+            v_quant(r)
 
         gu_t = {}
         sg_t = {}
@@ -247,74 +201,70 @@ def tile_blocksparsetop2mlphffp8_kernel(tc, hidden_states, w1_q, w1_s, w3_q, w3_
         def mm1(kind, w, c, tb):
             bank = psum.tile([P, 512], F32, name="%s_%d_%d" % (kind, c, tb), tag="GU")
             gu_t[(kind, c, tb)] = bank
+            cd, cs = cod_t[2 * c + (0 if w == 1 else 1)]
             for tau in range(4):
                 up, e = tau // 2, tau % 2
                 for g in range(2):
-                    cd, cs = cod_t[(w, c, up, g)]
+                    col = ((up * 2 + g) * 2 + e) * P
                     nc.tensor.matmul_mx(
                         out=bank[:, tau * P : (tau + 1) * P],
-                        lhsT=cd[:, e * P : (e + 1) * P].bitcast(FP8X4),
-                        lhsT_scale=cs[:, e * P : (e + 1) * P],
+                        lhsT=cd[:, col : col + P].bitcast(FP8X4),
+                        lhsT_scale=cs[:, col : col + P],
                         rhs=xc[:, g, tb * P : (tb + 1) * P].bitcast(FP8X4),
                         rhs_scale=xs[:, g, tb * P : (tb + 1) * P],
                         start=(g == 0),
                         stop=(g == 1),
                     )
 
-        def silu(c, tb):
-            sg = sgp.tile([P, P, 4], F32, name="sg_%d_%d" % (c, tb), tag="sg")
-            sg_t[(c, tb)] = sg
-            nc.scalar.activation(
-                out=sg[:], in_=gu_t[("g", c, tb)][:].rearrange("p (t r) -> p r t", t=4), func=ACT.Silu
-            )
+        def s_act(k):
+            c, h = k // 2, k % 2
+            sg = sgp.tile([P, 2, P, 4], F32, name="sg_%d" % k, tag="sg")
+            ub = sgp.tile([P, 2, P, 4], F32, name="ub_%d" % k, tag="ub")
+            sg_t[k] = (sg, ub)
+            for i in range(2):
+                tb = 2 * h + i
+                nc.scalar.activation(
+                    out=sg[:, i], in_=gu_t[("g", c, tb)][:].rearrange("p (t r) -> p r t", t=4), func=ACT.Silu
+                )
+                nc.scalar.copy(out=ub[:, i], in_=gu_t[("u", c, tb)][:].rearrange("p (t r) -> p r t", t=4))
 
-        def gate(c, tb):
+        def v_gate(k):
+            c, h = k // 2, k % 2
             if c not in fg_t:
-                fg_t[c] = fgp.tile([P, 4, P, 4], BF16, name="fg_%d" % c, tag="fg", align_bytes=64)
+                fg_t[c] = fgp.tile([P, 2, 1024], BF16, name="fg_%d" % c, tag="fg", align_bytes=64)
+            sg, ub = sg_t[k]
             nc.vector.tensor_tensor(
-                out=fg_t[c][:, tb, :, :],
-                in0=gu_t[("u", c, tb)][:].rearrange("p (t r) -> p r t", t=4),
-                in1=sg_t[(c, tb)][:],
+                out=fg_t[c][:, h, :],
+                in0=sg[:].rearrange("p a r t -> p (a r t)"),
+                in1=ub[:].rearrange("p a r t -> p (a r t)"),
                 op=ALU.mult,
             )
 
-        def qf(c):
+        def v_qf(c):
             nc.vector.quantize_mx(
-                out=fc[:, c, :].bitcast(FP8X4), scales=fs[:, c, :], in_=fg_t[c][:].rearrange("p a r t -> p (a r t)")
+                out=fc[:, c, :].bitcast(FP8X4), scales=fs[:, c, :], in_=fg_t[c][:].rearrange("p a x -> p (a x)")
             )
 
-        lag = []
         acc_t = {}
         for k in range(21):
             r = k + LA
             if r < 21:
                 t_run(r)
-                emit_exits(r)
-            for item in lag:
-                gate(item[0], item[1])
-                if item[2]:
-                    qf(item[0])
-            lag = []
+                s_copies(r)
+                v_scale(r)
+            if 1 <= k <= 14:
+                v_gate(k - 1)
             if k < 14:
                 c, h = k // 2, k % 2
-                a, b = 2 * h, 2 * h + 1
-                for tb in (a, b):
+                for tb in (2 * h, 2 * h + 1):
                     mm1("g", 1, c, tb)
                     mm1("u", 3, c, tb)
-                silu(c, a)
-                if r < 21:
-                    late_s(r)
-                silu(c, b)
-                if r < 21:
-                    for i in range(4):
-                        q(r, i)
-                gate(c, a)
-                lag.append((c, b, h == 1))
+                s_act(k)
             else:
                 j = k - 14
-                for u2 in (units2[2 * j], units2[2 * j + 1]):
+                cd, cs = cod_t[k]
+                for i, u2 in enumerate((units2[2 * j], units2[2 * j + 1])):
                     hh, c = u2
-                    wc, ws = w2c_t[u2]
                     for tb in range(4):
                         if c == 0:
                             acc_t[(hh, tb)] = psum.tile([P, 512], F32, name="acc_%d_%d" % (hh, tb), tag="GU")
@@ -323,21 +273,21 @@ def tile_blocksparsetop2mlphffp8_kernel(tc, hidden_states, w1_q, w1_s, w3_q, w3_
                             out=acc[:],
                             lhsT=fc[:, c, tb * P : (tb + 1) * P].bitcast(FP8X4),
                             lhsT_scale=fs[:, c, tb * P : (tb + 1) * P],
-                            rhs=wc[:].bitcast(FP8X4),
-                            rhs_scale=ws[:],
+                            rhs=cd[:, 512 * i : 512 * (i + 1)].bitcast(FP8X4),
+                            rhs_scale=cs[:, 512 * i : 512 * (i + 1)],
                             start=(c == 0),
                             stop=(c == 6),
                         )
                         if c == 6:
                             ob = obp.tile([P, 512], F32, name="ob_%d_%d" % (hh, tb), tag="ob")
-                            if tb % 2 == 0:
+                            if tb % 2 == 0 or hh == 0:
                                 nc.scalar.copy(out=ob[:], in_=acc[:])
                             else:
                                 nc.vector.tensor_copy(out=ob[:], in_=acc[:])
                             nc.sync.dma_start(
                                 out=out[tb * P : (tb + 1) * P, hh * 512 : (hh + 1) * 512], in_=ob[:]
                             )
-                if r < 21:
-                    late_s(r)
-                    for i in range(4):
-                        q(r, i)
+            if r < 21:
+                v_quant(r)
+            if 1 <= k <= 14 and k % 2 == 0:
+                v_qf((k - 1) // 2)

@@ -16,7 +16,7 @@ P = 128
 FLOPS = 2 * T * H * F * 3
 
 LA = 3
-RAW_BUFS = 18
+RAW_BUFS = 16
 
 
 def tile_blocksparsetop2mlphffp8_kernel(tc, hidden_states, w1_q, w1_s, w3_q, w3_s, w2_q, w2_s, out):
@@ -24,10 +24,10 @@ def tile_blocksparsetop2mlphffp8_kernel(tc, hidden_states, w1_q, w1_s, w3_q, w3_
     with ExitStack() as ctx:
         const = ctx.enter_context(tc.tile_pool(name="const", bufs=1))
         rawp = ctx.enter_context(tc.tile_pool(name="rawp", bufs=RAW_BUFS))
-        grpp = ctx.enter_context(tc.tile_pool(name="grpp", bufs=4))
+        grpp = ctx.enter_context(tc.tile_pool(name="grpp", bufs=3))
         codp = ctx.enter_context(tc.tile_pool(name="codp", bufs=7))
         sgp = ctx.enter_context(tc.tile_pool(name="sgp", bufs=3))
-        fgp = ctx.enter_context(tc.tile_pool(name="fgp", bufs=2))
+        fgp = ctx.enter_context(tc.tile_pool(name="fgp", bufs=7))
         obp = ctx.enter_context(tc.tile_pool(name="obp", bufs=4))
         psum = ctx.enter_context(tc.psum_pool(name="psum", bufs=4))
         ctx.enter_context(tc.manual_schedule())
@@ -83,7 +83,7 @@ def tile_blocksparsetop2mlphffp8_kernel(tc, hidden_states, w1_q, w1_s, w3_q, w3_
         units2 = [(hh, c) for hh in range(2) for c in range(7)]
         for j in range(7):
             runs.append([((2,) + u + (q,), (2,) + u) for u in (units2[2 * j], units2[2 * j + 1]) for q in range(2)])
-        load_order = [("x", 0), ("x", 1)]
+        load_order = [(1, 0, 0), (1, 0, 1), ("x", 0), ("x", 1)]
         for r in runs:
             for bk, ru in r:
                 if ru not in load_order:
@@ -118,8 +118,8 @@ def tile_blocksparsetop2mlphffp8_kernel(tc, hidden_states, w1_q, w1_s, w3_q, w3_
                 nc.sync.dma_start(out=dst, in_=src)
                 state["loaded"] += 1
 
-        def t_run(r):
-            for bk, ru in runs[r]:
+        def t_banks(r, lo, n):
+            for bk, ru in runs[r][lo : lo + n]:
                 bank = psum.tile([P, 512], F32, name="T_" + nm(bk), tag="T")
                 bank_t[bk] = bank
                 rf = raw_t[ru][:].bitcast(F32)
@@ -132,40 +132,45 @@ def tile_blocksparsetop2mlphffp8_kernel(tc, hidden_states, w1_q, w1_s, w3_q, w3_
                         nc.tensor.transpose(
                             bank[:, (2 * u + b) * P : (2 * u + b + 1) * P], rf[:, col : col + P], ident[:]
                         )
-            state["used"] += 2
+            state["used"] += n // 2
             load_upto(state["used"] + RAW_BUFS)
 
-        def s_copies(r):
-            grp = grpp.tile([P, 4096], BF16, name="grp_%d" % r, tag="grp", align_bytes=64)
-            grp_t[r] = grp
-            gf = grp[:].bitcast(F32)
-            for i in range(4):
+        def s_copies(r, lo, n):
+            if lo == 0:
+                grp_t[r] = grpp.tile([P, 4096], BF16, name="grp_%d" % r, tag="grp", align_bytes=64)
+            gf = grp_t[r][:].bitcast(F32)
+            for i in range(lo, lo + n):
                 bk, ru = runs[r][i]
                 nc.scalar.copy(
                     out=gf[:, 512 * i : 512 * (i + 1)].rearrange("p (n u) -> p n u", u=2),
                     in_=bank_t[bk][:].rearrange("p (u n) -> p n u", u=2),
                 )
 
-        def v_scale(r):
-            grp = grp_t[r]
+        def v_scale(r, lo, n):
             kind = runs[r][0][0][0]
-            if kind == 2:
-                j = r - 14
-                view = grp[:].rearrange("p (j n x) -> p j n x", n=128, x=4)
-                tab = tabs[2][:, 8 * j : 8 * (j + 1), :].unsqueeze(2).to_broadcast([P, 8, 128, 4])
-            else:
-                c = runs[r][0][0][1]
-                view = grp[:].rearrange("p (j n x) -> p j n x", n=64, x=4)
-                tab = tabs[kind][:, 16 * c : 16 * (c + 1), :].unsqueeze(2).to_broadcast([P, 16, 64, 4])
+            cols = 128 if kind == 2 else 64
+            per = 256 // cols
+            first = (r - 14 if kind == 2 else runs[r][0][0][1]) * 4 * per + lo * per
+            view = grp_t[r][:, 1024 * lo : 1024 * (lo + n)].rearrange("p (j n x) -> p j n x", n=cols, x=4)
+            tab = tabs[kind][:, first : first + n * per, :].unsqueeze(2).to_broadcast([P, n * per, cols, 4])
             nc.vector.tensor_tensor(out=view, in0=view, in1=tab, op=ALU.mult)
 
-        def v_quant(r):
-            cd = codp.tile([P, 1024], U32, name="cod_%d" % r, tag="cod", align_bytes=64)
-            cs = codp.tile([P, 1024], U8, name="cos_%d" % r, tag="cos", align_bytes=64)
-            cod_t[r] = (cd, cs)
-            nc.vector.quantize_mx(out=cd[:].bitcast(FP8X4), scales=cs[:], in_=grp_t[r][:])
+        def v_quant(r, lo, n):
+            if r not in cod_t:
+                cd = codp.tile([P, 1024], U32, name="cod_%d" % r, tag="cod", align_bytes=64)
+                cs = codp.tile([P, 1024], U8, name="cos_%d" % r, tag="cos", align_bytes=64)
+                cod_t[r] = (cd, cs)
+            cd, cs = cod_t[r]
+            sl = slice(256 * lo, 256 * (lo + n))
+            nc.vector.quantize_mx(
+                out=cd[:, sl].bitcast(FP8X4), scales=cs[:, sl], in_=grp_t[r][:, 1024 * lo : 1024 * (lo + n)]
+            )
 
         load_upto(RAW_BUFS)
+        t_banks(0, 0, 4)
+        s_copies(0, 0, 4)
+        v_scale(0, 0, 2)
+        v_scale(0, 2, 2)
         xgf = xg[:].bitcast(F32).rearrange("p (g t r u) -> p t g r u", g=2, t=4, r=P, u=2)
         xbanks = []
         for t in range(4):
@@ -178,21 +183,21 @@ def tile_blocksparsetop2mlphffp8_kernel(tc, hidden_states, w1_q, w1_s, w3_q, w3_
                     nc.tensor.transpose(bank[:, (2 * u + g) * P : (2 * u + g + 1) * P], rf[:, col : col + P], ident[:])
         for t in range(4):
             src = xbanks[t][:].rearrange("p (u g r) -> p g r u", u=2, g=2, r=P)
-            if t % 2:
-                nc.scalar.copy(out=xgf[:, t], in_=src)
-            else:
-                nc.vector.tensor_copy(out=xgf[:, t], in_=src)
+            nc.scalar.copy(out=xgf[:, t], in_=src)
+        v_quant(0, 0, 2)
+        v_quant(0, 2, 2)
         for g in range(2):
             nc.vector.quantize_mx(
                 out=xc[:, g, :].bitcast(FP8X4), scales=xs[:, g, :], in_=xg[:, 2048 * g : 2048 * (g + 1)]
             )
-        state["used"] = 2
+        state["used"] += 2
+        load_upto(state["used"] + RAW_BUFS)
 
-        for r in range(LA):
-            t_run(r)
-            s_copies(r)
-            v_scale(r)
-            v_quant(r)
+        for r in range(1, LA):
+            t_banks(r, 0, 4)
+            s_copies(r, 0, 4)
+            v_scale(r, 0, 4)
+            v_quant(r, 0, 4)
 
         gu_t = {}
         sg_t = {}
@@ -216,17 +221,17 @@ def tile_blocksparsetop2mlphffp8_kernel(tc, hidden_states, w1_q, w1_s, w3_q, w3_
                         stop=(g == 1),
                     )
 
-        def s_act(k):
-            c, h = k // 2, k % 2
-            sg = sgp.tile([P, 2, P, 4], F32, name="sg_%d" % k, tag="sg")
-            ub = sgp.tile([P, 2, P, 4], F32, name="ub_%d" % k, tag="ub")
-            sg_t[k] = (sg, ub)
-            for i in range(2):
-                tb = 2 * h + i
-                nc.scalar.activation(
-                    out=sg[:, i], in_=gu_t[("g", c, tb)][:].rearrange("p (t r) -> p r t", t=4), func=ACT.Silu
-                )
-                nc.scalar.copy(out=ub[:, i], in_=gu_t[("u", c, tb)][:].rearrange("p (t r) -> p r t", t=4))
+        def s_act(k, i):
+            c, tb = k // 2, 2 * (k % 2) + i
+            if i == 0:
+                sg_new = sgp.tile([P, 2, P, 4], F32, name="sg_%d" % k, tag="sg")
+                ub_new = sgp.tile([P, 2, P, 4], F32, name="ub_%d" % k, tag="ub")
+                sg_t[k] = (sg_new, ub_new)
+            sg, ub = sg_t[k]
+            nc.scalar.activation(
+                out=sg[:, i], in_=gu_t[("g", c, tb)][:].rearrange("p (t r) -> p r t", t=4), func=ACT.Silu
+            )
+            nc.scalar.copy(out=ub[:, i], in_=gu_t[("u", c, tb)][:].rearrange("p (t r) -> p r t", t=4))
 
         def v_gate(k):
             c, h = k // 2, k % 2
@@ -246,48 +251,54 @@ def tile_blocksparsetop2mlphffp8_kernel(tc, hidden_states, w1_q, w1_s, w3_q, w3_
             )
 
         acc_t = {}
+
+        def mm2(k, i):
+            hh, c = units2[2 * (k - 14) + i]
+            cd, cs = cod_t[k]
+            for tb in range(4):
+                if c == 0:
+                    acc_t[(hh, tb)] = psum.tile([P, 512], F32, name="acc_%d_%d" % (hh, tb), tag="GU")
+                acc = acc_t[(hh, tb)]
+                nc.tensor.matmul_mx(
+                    out=acc[:],
+                    lhsT=fc[:, c, tb * P : (tb + 1) * P].bitcast(FP8X4),
+                    lhsT_scale=fs[:, c, tb * P : (tb + 1) * P],
+                    rhs=cd[:, 512 * i : 512 * (i + 1)].bitcast(FP8X4),
+                    rhs_scale=cs[:, 512 * i : 512 * (i + 1)],
+                    start=(c == 0),
+                    stop=(c == 6),
+                )
+                if c == 6:
+                    ob = obp.tile([P, 512], F32, name="ob_%d_%d" % (hh, tb), tag="ob")
+                    if tb % 2 == 0 or hh == 0:
+                        nc.scalar.copy(out=ob[:], in_=acc[:])
+                    else:
+                        nc.vector.tensor_copy(out=ob[:], in_=acc[:])
+                    nc.sync.dma_start(out=out[tb * P : (tb + 1) * P, hh * 512 : (hh + 1) * 512], in_=ob[:])
+
         for k in range(21):
             r = k + LA
-            if r < 21:
-                t_run(r)
-                s_copies(r)
-                v_scale(r)
+            for i in range(2):
+                if r < 21:
+                    t_banks(r, 2 * i, 2)
+                    s_copies(r, 2 * i, 2)
+                    if r == 20:
+                        v_scale(r, 2 * i, 2)
+                if k < 14:
+                    mm1("g", 1, k // 2, 2 * (k % 2) + i)
+                    mm1("u", 3, k // 2, 2 * (k % 2) + i)
+                    s_act(k, i)
+                else:
+                    mm2(k, i)
+            if r < 20:
+                v_scale(r, 0, 4)
             if 1 <= k <= 14:
                 v_gate(k - 1)
-            if k < 14:
-                c, h = k // 2, k % 2
-                for tb in (2 * h, 2 * h + 1):
-                    mm1("g", 1, c, tb)
-                    mm1("u", 3, c, tb)
-                s_act(k)
-            else:
-                j = k - 14
-                cd, cs = cod_t[k]
-                for i, u2 in enumerate((units2[2 * j], units2[2 * j + 1])):
-                    hh, c = u2
-                    for tb in range(4):
-                        if c == 0:
-                            acc_t[(hh, tb)] = psum.tile([P, 512], F32, name="acc_%d_%d" % (hh, tb), tag="GU")
-                        acc = acc_t[(hh, tb)]
-                        nc.tensor.matmul_mx(
-                            out=acc[:],
-                            lhsT=fc[:, c, tb * P : (tb + 1) * P].bitcast(FP8X4),
-                            lhsT_scale=fs[:, c, tb * P : (tb + 1) * P],
-                            rhs=cd[:, 512 * i : 512 * (i + 1)].bitcast(FP8X4),
-                            rhs_scale=cs[:, 512 * i : 512 * (i + 1)],
-                            start=(c == 0),
-                            stop=(c == 6),
-                        )
-                        if c == 6:
-                            ob = obp.tile([P, 512], F32, name="ob_%d_%d" % (hh, tb), tag="ob")
-                            if tb % 2 == 0 or hh == 0:
-                                nc.scalar.copy(out=ob[:], in_=acc[:])
-                            else:
-                                nc.vector.tensor_copy(out=ob[:], in_=acc[:])
-                            nc.sync.dma_start(
-                                out=out[tb * P : (tb + 1) * P, hh * 512 : (hh + 1) * 512], in_=ob[:]
-                            )
-            if r < 21:
-                v_quant(r)
-            if 1 <= k <= 14 and k % 2 == 0:
-                v_qf((k - 1) // 2)
+            if 13 <= k <= 16:
+                for c in range(2 * (k - 13), min(2 * (k - 13) + 2, 7)):
+                    v_qf(c)
+            if r == 20:
+                v_quant(r, 0, 2)
+                v_quant(r, 2, 2)
+            elif r < 21:
+                v_quant(r, 0, 4)

@@ -118,8 +118,8 @@ def tile_blocksparsetop2mlphffp8_kernel(tc, hidden_states, w1_q, w1_s, w3_q, w3_
                 nc.sync.dma_start(out=dst, in_=src)
                 state["loaded"] += 1
 
-        def t_banks(r, lo, n):
-            for bk, ru in runs[r][lo : lo + n]:
+        def t_run(r):
+            for bk, ru in runs[r]:
                 bank = psum.tile([P, 512], F32, name="T_" + nm(bk), tag="T")
                 bank_t[bk] = bank
                 rf = raw_t[ru][:].bitcast(F32)
@@ -132,14 +132,14 @@ def tile_blocksparsetop2mlphffp8_kernel(tc, hidden_states, w1_q, w1_s, w3_q, w3_
                         nc.tensor.transpose(
                             bank[:, (2 * u + b) * P : (2 * u + b + 1) * P], rf[:, col : col + P], ident[:]
                         )
-            state["used"] += n // 2
+            state["used"] += 2
             load_upto(state["used"] + RAW_BUFS)
 
-        def s_copies(r, lo, n):
-            if lo == 0:
-                grp_t[r] = grpp.tile([P, 4096], BF16, name="grp_%d" % r, tag="grp", align_bytes=64)
-            gf = grp_t[r][:].bitcast(F32)
-            for i in range(lo, lo + n):
+        def s_copies(r):
+            grp = grpp.tile([P, 4096], BF16, name="grp_%d" % r, tag="grp", align_bytes=64)
+            grp_t[r] = grp
+            gf = grp[:].bitcast(F32)
+            for i in range(4):
                 bk, ru = runs[r][i]
                 nc.scalar.copy(
                     out=gf[:, 512 * i : 512 * (i + 1)].rearrange("p (n u) -> p n u", u=2),
@@ -167,8 +167,8 @@ def tile_blocksparsetop2mlphffp8_kernel(tc, hidden_states, w1_q, w1_s, w3_q, w3_
             )
 
         load_upto(RAW_BUFS)
-        t_banks(0, 0, 4)
-        s_copies(0, 0, 4)
+        t_run(0)
+        s_copies(0)
         v_scale(0, 0, 2)
         v_scale(0, 2, 2)
         xgf = xg[:].bitcast(F32).rearrange("p (g t r u) -> p t g r u", g=2, t=4, r=P, u=2)
@@ -194,8 +194,8 @@ def tile_blocksparsetop2mlphffp8_kernel(tc, hidden_states, w1_q, w1_s, w3_q, w3_
         load_upto(state["used"] + RAW_BUFS)
 
         for r in range(1, LA):
-            t_banks(r, 0, 4)
-            s_copies(r, 0, 4)
+            t_run(r)
+            s_copies(r)
             v_scale(r, 0, 4)
             v_quant(r, 0, 4)
 
@@ -221,29 +221,27 @@ def tile_blocksparsetop2mlphffp8_kernel(tc, hidden_states, w1_q, w1_s, w3_q, w3_
                         stop=(g == 1),
                     )
 
-        def s_act(k, i):
-            c, tb = k // 2, 2 * (k % 2) + i
-            if i == 0:
-                sg_new = sgp.tile([P, 2, P, 4], F32, name="sg_%d" % k, tag="sg")
-                ub_new = sgp.tile([P, 2, P, 4], F32, name="ub_%d" % k, tag="ub")
-                sg_t[k] = (sg_new, ub_new)
-            sg, ub = sg_t[k]
-            nc.scalar.activation(
-                out=sg[:, i], in_=gu_t[("g", c, tb)][:].rearrange("p (t r) -> p r t", t=4), func=ACT.Silu
-            )
-            nc.scalar.copy(out=ub[:, i], in_=gu_t[("u", c, tb)][:].rearrange("p (t r) -> p r t", t=4))
+        def s_act(k):
+            c, h = k // 2, k % 2
+            sg = sgp.tile([P, 2, P, 4], F32, name="sg_%d" % k, tag="sg")
+            sg_t[k] = sg
+            for i in range(2):
+                tb = 2 * h + i
+                nc.scalar.activation(
+                    out=sg[:, i], in_=gu_t[("g", c, tb)][:].rearrange("p (t r) -> p r t", t=4), func=ACT.Silu
+                )
 
         def v_gate(k):
             c, h = k // 2, k % 2
             if c not in fg_t:
                 fg_t[c] = fgp.tile([P, 2, 1024], BF16, name="fg_%d" % c, tag="fg", align_bytes=64)
-            sg, ub = sg_t[k]
-            nc.vector.tensor_tensor(
-                out=fg_t[c][:, h, :],
-                in0=sg[:].rearrange("p a r t -> p (a r t)"),
-                in1=ub[:].rearrange("p a r t -> p (a r t)"),
-                op=ALU.mult,
-            )
+            for i in range(2):
+                nc.vector.tensor_tensor(
+                    out=fg_t[c][:, h, 512 * i : 512 * (i + 1)].rearrange("p (r t) -> p r t", t=4),
+                    in0=gu_t[("u", c, 2 * h + i)][:].rearrange("p (t r) -> p r t", t=4),
+                    in1=sg_t[k][:, i],
+                    op=ALU.mult,
+                )
 
         def v_qf(c):
             nc.vector.quantize_mx(
@@ -251,54 +249,50 @@ def tile_blocksparsetop2mlphffp8_kernel(tc, hidden_states, w1_q, w1_s, w3_q, w3_
             )
 
         acc_t = {}
-
-        def mm2(k, i):
-            hh, c = units2[2 * (k - 14) + i]
-            cd, cs = cod_t[k]
-            for tb in range(4):
-                if c == 0:
-                    acc_t[(hh, tb)] = psum.tile([P, 512], F32, name="acc_%d_%d" % (hh, tb), tag="GU")
-                acc = acc_t[(hh, tb)]
-                nc.tensor.matmul_mx(
-                    out=acc[:],
-                    lhsT=fc[:, c, tb * P : (tb + 1) * P].bitcast(FP8X4),
-                    lhsT_scale=fs[:, c, tb * P : (tb + 1) * P],
-                    rhs=cd[:, 512 * i : 512 * (i + 1)].bitcast(FP8X4),
-                    rhs_scale=cs[:, 512 * i : 512 * (i + 1)],
-                    start=(c == 0),
-                    stop=(c == 6),
-                )
-                if c == 6:
-                    ob = obp.tile([P, 512], F32, name="ob_%d_%d" % (hh, tb), tag="ob")
-                    if tb % 2 == 0 or hh == 0:
-                        nc.scalar.copy(out=ob[:], in_=acc[:])
-                    else:
-                        nc.vector.tensor_copy(out=ob[:], in_=acc[:])
-                    nc.sync.dma_start(out=out[tb * P : (tb + 1) * P, hh * 512 : (hh + 1) * 512], in_=ob[:])
-
         for k in range(21):
             r = k + LA
-            for i in range(2):
-                if r < 21:
-                    t_banks(r, 2 * i, 2)
-                    s_copies(r, 2 * i, 2)
-                    if r == 20:
-                        v_scale(r, 2 * i, 2)
-                if k < 14:
-                    mm1("g", 1, k // 2, 2 * (k % 2) + i)
-                    mm1("u", 3, k // 2, 2 * (k % 2) + i)
-                    s_act(k, i)
-                else:
-                    mm2(k, i)
-            if r < 20:
-                v_scale(r, 0, 4)
+            if r < 21:
+                t_run(r)
+                s_copies(r)
             if 1 <= k <= 14:
                 v_gate(k - 1)
             if 13 <= k <= 16:
                 for c in range(2 * (k - 13), min(2 * (k - 13) + 2, 7)):
                     v_qf(c)
-            if r == 20:
-                v_quant(r, 0, 2)
-                v_quant(r, 2, 2)
-            elif r < 21:
-                v_quant(r, 0, 4)
+            if LA < r <= 21:
+                v_quant(r - 1, 0, 4)
+            if r < 21:
+                v_scale(r, 0, 4)
+            if k < 14:
+                c, h = k // 2, k % 2
+                for tb in (2 * h, 2 * h + 1):
+                    mm1("g", 1, c, tb)
+                    mm1("u", 3, c, tb)
+                s_act(k)
+            else:
+                j = k - 14
+                cd, cs = cod_t[k]
+                for i, u2 in enumerate((units2[2 * j], units2[2 * j + 1])):
+                    hh, c = u2
+                    for tb in range(4):
+                        if c == 0:
+                            acc_t[(hh, tb)] = psum.tile([P, 512], F32, name="acc_%d_%d" % (hh, tb), tag="GU")
+                        acc = acc_t[(hh, tb)]
+                        nc.tensor.matmul_mx(
+                            out=acc[:],
+                            lhsT=fc[:, c, tb * P : (tb + 1) * P].bitcast(FP8X4),
+                            lhsT_scale=fs[:, c, tb * P : (tb + 1) * P],
+                            rhs=cd[:, 512 * i : 512 * (i + 1)].bitcast(FP8X4),
+                            rhs_scale=cs[:, 512 * i : 512 * (i + 1)],
+                            start=(c == 0),
+                            stop=(c == 6),
+                        )
+                        if c == 6:
+                            ob = obp.tile([P, 512], F32, name="ob_%d_%d" % (hh, tb), tag="ob")
+                            if tb % 2 == 0 or hh == 0:
+                                nc.scalar.copy(out=ob[:], in_=acc[:])
+                            else:
+                                nc.vector.tensor_copy(out=ob[:], in_=acc[:])
+                            nc.sync.dma_start(
+                                out=out[tb * P : (tb + 1) * P, hh * 512 : (hh + 1) * 512], in_=ob[:]
+                            )

@@ -28,6 +28,7 @@ def tile_blocksparsetop2mlphffp8_kernel(tc, hidden_states, w1_q, w1_s, w3_q, w3_
         codp = ctx.enter_context(tc.tile_pool(name="codp", bufs=7))
         sgp = ctx.enter_context(tc.tile_pool(name="sgp", bufs=3))
         fgp = ctx.enter_context(tc.tile_pool(name="fgp", bufs=7))
+        fplp = ctx.enter_context(tc.tile_pool(name="fplp", bufs=2))
         obp = ctx.enter_context(tc.tile_pool(name="obp", bufs=4))
         psum = ctx.enter_context(tc.psum_pool(name="psum", bufs=4))
         ctx.enter_context(tc.manual_schedule())
@@ -207,45 +208,44 @@ def tile_blocksparsetop2mlphffp8_kernel(tc, hidden_states, w1_q, w1_s, w3_q, w3_
             bank = psum.tile([P, 512], F32, name="%s_%d_%d" % (kind, c, tb), tag="GU")
             gu_t[(kind, c, tb)] = bank
             cd, cs = cod_t[2 * c + (0 if w == 1 else 1)]
-            for tau in range(4):
-                up, e = tau // 2, tau % 2
-                for g in range(2):
-                    col = ((up * 2 + g) * 2 + e) * P
-                    nc.tensor.matmul_mx(
-                        out=bank[:, tau * P : (tau + 1) * P],
-                        lhsT=cd[:, col : col + P].bitcast(FP8X4),
-                        lhsT_scale=cs[:, col : col + P],
-                        rhs=xc[:, g, tb * P : (tb + 1) * P].bitcast(FP8X4),
-                        rhs_scale=xs[:, g, tb * P : (tb + 1) * P],
-                        start=(g == 0),
-                        stop=(g == 1),
-                    )
+            up, e = tb // 2, tb % 2
+            for g in range(2):
+                col = ((up * 2 + g) * 2 + e) * P
+                nc.tensor.matmul_mx(
+                    out=bank[:],
+                    lhsT=cd[:, col : col + P].bitcast(FP8X4),
+                    lhsT_scale=cs[:, col : col + P],
+                    rhs=xc[:, g, :].bitcast(FP8X4),
+                    rhs_scale=xs[:, g, :],
+                    start=(g == 0),
+                    stop=(g == 1),
+                )
 
         def s_act(k):
             c, h = k // 2, k % 2
-            sg = sgp.tile([P, 2, P, 4], F32, name="sg_%d" % k, tag="sg")
+            sg = sgp.tile([P, 2, 512], F32, name="sg_%d" % k, tag="sg")
             sg_t[k] = sg
             for i in range(2):
-                tb = 2 * h + i
-                nc.scalar.activation(
-                    out=sg[:, i], in_=gu_t[("g", c, tb)][:].rearrange("p (t r) -> p r t", t=4), func=ACT.Silu
-                )
+                nc.scalar.activation(out=sg[:, i, :], in_=gu_t[("g", c, 2 * h + i)][:], func=ACT.Silu)
+
+        fpl_t = {}
 
         def v_gate(k):
             c, h = k // 2, k % 2
-            if c not in fg_t:
-                fg_t[c] = fgp.tile([P, 2, 1024], BF16, name="fg_%d" % c, tag="fg", align_bytes=64)
+            if c not in fpl_t:
+                fpl_t[c] = fplp.tile([P, 4, 512], BF16, name="fpl_%d" % c, tag="fpl")
             for i in range(2):
                 nc.vector.tensor_tensor(
-                    out=fg_t[c][:, h, 512 * i : 512 * (i + 1)].rearrange("p (r t) -> p r t", t=4),
-                    in0=gu_t[("u", c, 2 * h + i)][:].rearrange("p (t r) -> p r t", t=4),
-                    in1=sg_t[k][:, i],
-                    op=ALU.mult,
+                    out=fpl_t[c][:, 2 * h + i, :], in0=gu_t[("u", c, 2 * h + i)][:], in1=sg_t[k][:, i, :], op=ALU.mult
                 )
+
+        def s_regroup(c):
+            fg_t[c] = fgp.tile([P, 512, 4], BF16, name="fg_%d" % c, tag="fg", align_bytes=64)
+            nc.scalar.copy(out=fg_t[c][:], in_=fpl_t[c][:].rearrange("p t r -> p r t"))
 
         def v_qf(c):
             nc.vector.quantize_mx(
-                out=fc[:, c, :].bitcast(FP8X4), scales=fs[:, c, :], in_=fg_t[c][:].rearrange("p a x -> p (a x)")
+                out=fc[:, c, :].bitcast(FP8X4), scales=fs[:, c, :], in_=fg_t[c][:].rearrange("p r t -> p (r t)")
             )
 
         acc_t = {}
@@ -269,7 +269,9 @@ def tile_blocksparsetop2mlphffp8_kernel(tc, hidden_states, w1_q, w1_s, w3_q, w3_
                     mm1("g", 1, c, tb)
                     mm1("u", 3, c, tb)
                 s_act(k)
-            else:
+            if 2 <= k <= 14 and k % 2 == 0:
+                s_regroup(k // 2 - 1)
+            if k >= 14:
                 j = k - 14
                 cd, cs = cod_t[k]
                 for i, u2 in enumerate((units2[2 * j], units2[2 * j + 1])):

@@ -28,7 +28,6 @@ def tile_blocksparsetop2mlphffp8_kernel(tc, hidden_states, w1_q, w1_s, w3_q, w3_
         codp = ctx.enter_context(tc.tile_pool(name="codp", bufs=7))
         sgp = ctx.enter_context(tc.tile_pool(name="sgp", bufs=3))
         fgp = ctx.enter_context(tc.tile_pool(name="fgp", bufs=7))
-        fplp = ctx.enter_context(tc.tile_pool(name="fplp", bufs=2))
         obp = ctx.enter_context(tc.tile_pool(name="obp", bufs=4))
         psum = ctx.enter_context(tc.psum_pool(name="psum", bufs=4))
         ctx.enter_context(tc.manual_schedule())
@@ -40,17 +39,33 @@ def tile_blocksparsetop2mlphffp8_kernel(tc, hidden_states, w1_q, w1_s, w3_q, w3_
         nc.vector.memset(warm_in[:], 0.0)
         nc.scalar.activation(out=warm_out[:], in_=warm_in[:], func=ACT.Silu)
 
-        sraw = const.tile([P, 672], BF16, name="sraw")
+        sraw = const.tile([P, 768], BF16, name="sraw")
+        nc.vector.memset(sraw[:], 0.0)
+        ones = const.tile([P, P], BF16, name="ones")
+        nc.vector.memset(ones[:], 1.0)
         for i, sc in enumerate((w1_s, w3_s, w2_s)):
             nc.scalar.dma_start(
-                out=sraw[:, 224 * i : 224 * (i + 1)],
-                in_=sc.rearrange("a b -> (a b)").partition_broadcast(P),
+                out=sraw[0:1, 224 * i : 224 * (i + 1)], in_=sc.rearrange("a b -> (a b)").unsqueeze(0)
             )
+        spread_a = psum.tile([P, 512], F32, name="spread_a", tag="T")
+        spread_b = psum.tile([P, 512], F32, name="spread_b", tag="T")
+        nc.tensor.matmul(out=spread_a[:], lhsT=ones[:], rhs=sraw[:, 0:512], start=True, stop=True)
+        nc.tensor.matmul(out=spread_b[:, 0:256], lhsT=ones[:], rhs=sraw[:, 512:768], start=True, stop=True)
         scb = const.tile([P, 336, 2], BF16, name="scb")
         for half in range(2):
             rows = slice(64 * half, 64 * half + 64)
-            src = sraw[rows, :].rearrange("p (m h) -> p m h", h=2)[:, :, half : half + 1]
-            nc.vector.tensor_copy(out=scb[rows, :, :], in_=src.to_broadcast([64, 336, 2]))
+            nc.vector.tensor_copy(
+                out=scb[rows, 0:256, :],
+                in_=spread_a[rows, :]
+                .rearrange("p (m h) -> p m h", h=2)[:, :, half : half + 1]
+                .to_broadcast([64, 256, 2]),
+            )
+            nc.vector.tensor_copy(
+                out=scb[rows, 256:336, :],
+                in_=spread_b[rows, 0:160]
+                .rearrange("p (m h) -> p m h", h=2)[:, :, half : half + 1]
+                .to_broadcast([64, 80, 2]),
+            )
         tabs = {}
         for i, w in enumerate((1, 3)):
             tab = const.tile([P, 112, 4], BF16, name="tab%d" % w)
@@ -208,44 +223,45 @@ def tile_blocksparsetop2mlphffp8_kernel(tc, hidden_states, w1_q, w1_s, w3_q, w3_
             bank = psum.tile([P, 512], F32, name="%s_%d_%d" % (kind, c, tb), tag="GU")
             gu_t[(kind, c, tb)] = bank
             cd, cs = cod_t[2 * c + (0 if w == 1 else 1)]
-            up, e = tb // 2, tb % 2
-            for g in range(2):
-                col = ((up * 2 + g) * 2 + e) * P
-                nc.tensor.matmul_mx(
-                    out=bank[:],
-                    lhsT=cd[:, col : col + P].bitcast(FP8X4),
-                    lhsT_scale=cs[:, col : col + P],
-                    rhs=xc[:, g, :].bitcast(FP8X4),
-                    rhs_scale=xs[:, g, :],
-                    start=(g == 0),
-                    stop=(g == 1),
-                )
+            for tau in range(4):
+                up, e = tau // 2, tau % 2
+                for g in range(2):
+                    col = ((up * 2 + g) * 2 + e) * P
+                    nc.tensor.matmul_mx(
+                        out=bank[:, tau * P : (tau + 1) * P],
+                        lhsT=cd[:, col : col + P].bitcast(FP8X4),
+                        lhsT_scale=cs[:, col : col + P],
+                        rhs=xc[:, g, tb * P : (tb + 1) * P].bitcast(FP8X4),
+                        rhs_scale=xs[:, g, tb * P : (tb + 1) * P],
+                        start=(g == 0),
+                        stop=(g == 1),
+                    )
 
         def s_act(k):
             c, h = k // 2, k % 2
-            sg = sgp.tile([P, 2, 512], F32, name="sg_%d" % k, tag="sg")
+            sg = sgp.tile([P, 2, P, 4], F32, name="sg_%d" % k, tag="sg")
             sg_t[k] = sg
             for i in range(2):
-                nc.scalar.activation(out=sg[:, i, :], in_=gu_t[("g", c, 2 * h + i)][:], func=ACT.Silu)
-
-        fpl_t = {}
+                tb = 2 * h + i
+                nc.scalar.activation(
+                    out=sg[:, i], in_=gu_t[("g", c, tb)][:].rearrange("p (t r) -> p r t", t=4), func=ACT.Silu
+                )
 
         def v_gate(k):
             c, h = k // 2, k % 2
-            if c not in fpl_t:
-                fpl_t[c] = fplp.tile([P, 4, 512], BF16, name="fpl_%d" % c, tag="fpl")
+            if c not in fg_t:
+                fg_t[c] = fgp.tile([P, 2, 1024], BF16, name="fg_%d" % c, tag="fg", align_bytes=64)
             for i in range(2):
                 nc.vector.tensor_tensor(
-                    out=fpl_t[c][:, 2 * h + i, :], in0=gu_t[("u", c, 2 * h + i)][:], in1=sg_t[k][:, i, :], op=ALU.mult
+                    out=fg_t[c][:, h, 512 * i : 512 * (i + 1)].rearrange("p (r t) -> p r t", t=4),
+                    in0=gu_t[("u", c, 2 * h + i)][:].rearrange("p (t r) -> p r t", t=4),
+                    in1=sg_t[k][:, i],
+                    op=ALU.mult,
                 )
-
-        def s_regroup(c):
-            fg_t[c] = fgp.tile([P, 512, 4], BF16, name="fg_%d" % c, tag="fg", align_bytes=64)
-            nc.scalar.copy(out=fg_t[c][:], in_=fpl_t[c][:].rearrange("p t r -> p r t"))
 
         def v_qf(c):
             nc.vector.quantize_mx(
-                out=fc[:, c, :].bitcast(FP8X4), scales=fs[:, c, :], in_=fg_t[c][:].rearrange("p r t -> p (r t)")
+                out=fc[:, c, :].bitcast(FP8X4), scales=fs[:, c, :], in_=fg_t[c][:].rearrange("p a x -> p (a x)")
             )
 
         acc_t = {}
@@ -269,9 +285,7 @@ def tile_blocksparsetop2mlphffp8_kernel(tc, hidden_states, w1_q, w1_s, w3_q, w3_
                     mm1("g", 1, c, tb)
                     mm1("u", 3, c, tb)
                 s_act(k)
-            if 2 <= k <= 14 and k % 2 == 0:
-                s_regroup(k // 2 - 1)
-            if k >= 14:
+            else:
                 j = k - 14
                 cd, cs = cod_t[k]
                 for i, u2 in enumerate((units2[2 * j], units2[2 * j + 1])):

@@ -13,9 +13,10 @@ ALU = mybir.AluOpType
 
 T, H, F = 512, 1024, 3584
 P = 128
+CHUNKS = F // 512
 FLOPS = 2 * T * H * F * 3
 
-LA = 3
+AHEAD = 3
 RAW_BUFS = 16
 
 
@@ -23,15 +24,23 @@ def tile_blocksparsetop2mlphffp8_kernel(tc, hidden_states, w1_q, w1_s, w3_q, w3_
     nc = tc.nc
     with ExitStack() as ctx:
         const = ctx.enter_context(tc.tile_pool(name="const", bufs=1))
-        rawp = ctx.enter_context(tc.tile_pool(name="rawp", bufs=RAW_BUFS))
-        grpp = ctx.enter_context(tc.tile_pool(name="grpp", bufs=3))
-        codp = ctx.enter_context(tc.tile_pool(name="codp", bufs=7))
-        sgp = ctx.enter_context(tc.tile_pool(name="sgp", bufs=3))
-        fgp = ctx.enter_context(tc.tile_pool(name="fgp", bufs=7))
-        obp = ctx.enter_context(tc.tile_pool(name="obp", bufs=4))
+        raw_pool = ctx.enter_context(tc.tile_pool(name="raw_pool", bufs=RAW_BUFS))
+        grouped_pool = ctx.enter_context(tc.tile_pool(name="grouped_pool", bufs=3))
+        words_pool = ctx.enter_context(tc.tile_pool(name="words_pool", bufs=AHEAD + 4))
+        silu_pool = ctx.enter_context(tc.tile_pool(name="silu_pool", bufs=3))
+        fused_pool = ctx.enter_context(tc.tile_pool(name="fused_pool", bufs=CHUNKS))
+        out_pool = ctx.enter_context(tc.tile_pool(name="out_pool", bufs=4))
         psum = ctx.enter_context(tc.psum_pool(name="psum", bufs=4))
         ctx.enter_context(tc.manual_schedule())
 
+        factors_row = const.tile([P, 768], BF16, name="factors_row")
+        nc.vector.memset(factors_row[:], 0.0)
+        for i, table in enumerate((w1_s, w3_s, w2_s)):
+            nc.sync.dma_start(
+                out=factors_row[0:1, 224 * i : 224 * (i + 1)], in_=table.rearrange("a b -> (a b)").unsqueeze(0)
+            )
+        ones = const.tile([P, P], BF16, name="ones")
+        nc.vector.memset(ones[:], 1.0)
         ident = const.tile([P, P], F32, name="ident")
         make_identity(nc, ident[:])
         warm_in = const.tile([P, 1], F32, name="warm_in")
@@ -39,276 +48,282 @@ def tile_blocksparsetop2mlphffp8_kernel(tc, hidden_states, w1_q, w1_s, w3_q, w3_
         nc.vector.memset(warm_in[:], 0.0)
         nc.scalar.activation(out=warm_out[:], in_=warm_in[:], func=ACT.Silu)
 
-        sraw = const.tile([P, 768], BF16, name="sraw")
-        nc.vector.memset(sraw[:], 0.0)
-        ones = const.tile([P, P], BF16, name="ones")
-        nc.vector.memset(ones[:], 1.0)
-        for i, sc in enumerate((w1_s, w3_s, w2_s)):
-            nc.scalar.dma_start(
-                out=sraw[0:1, 224 * i : 224 * (i + 1)], in_=sc.rearrange("a b -> (a b)").unsqueeze(0)
-            )
         spread_a = psum.tile([P, 512], F32, name="spread_a", tag="T")
         spread_b = psum.tile([P, 512], F32, name="spread_b", tag="T")
-        nc.tensor.matmul(out=spread_a[:], lhsT=ones[:], rhs=sraw[:, 0:512], start=True, stop=True)
-        nc.tensor.matmul(out=spread_b[:, 0:256], lhsT=ones[:], rhs=sraw[:, 512:768], start=True, stop=True)
-        scb = const.tile([P, 336, 2], BF16, name="scb")
+        nc.tensor.matmul(out=spread_a[:], lhsT=ones[:], rhs=factors_row[:, 0:512], start=True, stop=True)
+        nc.tensor.matmul(out=spread_b[:, 0:256], lhsT=ones[:], rhs=factors_row[:, 512:768], start=True, stop=True)
+        pairs = const.tile([P, 336, 2], BF16, name="pairs")
         for half in range(2):
             rows = slice(64 * half, 64 * half + 64)
             nc.vector.tensor_copy(
-                out=scb[rows, 0:256, :],
+                out=pairs[rows, 0:256, :],
                 in_=spread_a[rows, :]
                 .rearrange("p (m h) -> p m h", h=2)[:, :, half : half + 1]
                 .to_broadcast([64, 256, 2]),
             )
             nc.vector.tensor_copy(
-                out=scb[rows, 256:336, :],
+                out=pairs[rows, 256:336, :],
                 in_=spread_b[rows, 0:160]
                 .rearrange("p (m h) -> p m h", h=2)[:, :, half : half + 1]
                 .to_broadcast([64, 80, 2]),
             )
-        tabs = {}
+        factor_tab = {}
         for i, w in enumerate((1, 3)):
             tab = const.tile([P, 112, 4], BF16, name="tab%d" % w)
-            tabs[w] = tab
+            factor_tab[w] = tab
             for g in range(2):
-                for e in range(2):
+                for h in range(2):
                     nc.vector.tensor_copy(
-                        out=tab[:].rearrange("p (a g h r) x -> p a g h r x", g=2, h=2, r=2)[:, :, g, e, :, :],
-                        in_=scb[:, 112 * i : 112 * (i + 1), :].rearrange(
+                        out=tab[:].rearrange("p (a g h r) x -> p a g h r x", g=2, h=2, r=2)[:, :, g, h, :, :],
+                        in_=pairs[:, 112 * i : 112 * (i + 1), :].rearrange(
                             "p (a r g u) e -> p a r g (u e)", r=2, g=2, u=2
                         )[:, :, :, g, :],
                     )
         tab2 = const.tile([P, 56, 4], BF16, name="tab2")
-        tabs[2] = tab2
+        factor_tab[2] = tab2
         for hh in range(2):
             nc.vector.tensor_copy(
                 out=tab2[:, 28 * hh : 28 * (hh + 1), :].rearrange("p (c b) x -> p c b x", b=4),
-                in_=scb[:, 224:336, :].rearrange("p (hh b c u) e -> p hh c b (u e)", hh=2, b=4, c=7, u=2)[:, hh],
+                in_=pairs[:, 224:336, :].rearrange("p (hh b c u) e -> p hh c b (u e)", hh=2, b=4, c=7, u=2)[:, hh],
             )
 
-        xg = const.tile([P, 4096], BF16, name="xg", align_bytes=64)
-        xc = const.tile([P, 2, 512], U32, name="xc", align_bytes=64)
-        xs = const.tile([P, 2, 512], U8, name="xs", align_bytes=64)
-        fc = const.tile([P, 7, 512], U32, name="fc", align_bytes=64)
-        fs = const.tile([P, 7, 512], U8, name="fs", align_bytes=64)
+        x_grouped = const.tile([P, 4096], BF16, name="x_grouped", align_bytes=64)
+        x_words = const.tile([P, 2, 512], U32, name="x_words", align_bytes=64)
+        x_scales = const.tile([P, 2, 512], U8, name="x_scales", align_bytes=64)
+        f_words = const.tile([P, CHUNKS, 512], U32, name="f_words", align_bytes=64)
+        f_scales = const.tile([P, CHUNKS, 512], U8, name="f_scales", align_bytes=64)
 
         runs = []
-        for c in range(7):
+        for c in range(CHUNKS):
             for w in (1, 3):
-                runs.append([((w, c, up, g), (w, c, up)) for up in range(2) for g in range(2)])
-        units2 = [(hh, c) for hh in range(2) for c in range(7)]
-        for j in range(7):
+                runs.append([((w, c, a, g), (w, c, a)) for a in range(2) for g in range(2)])
+        units2 = [(hh, c) for hh in range(2) for c in range(CHUNKS)]
+        for j in range(CHUNKS):
             runs.append([((2,) + u + (q,), (2,) + u) for u in (units2[2 * j], units2[2 * j + 1]) for q in range(2)])
+        n_runs = len(runs)
         load_order = [(1, 0, 0), (1, 0, 1), ("x", 0), ("x", 1)]
-        for r in runs:
-            for bk, ru in r:
-                if ru not in load_order:
-                    load_order.append(ru)
+        for run in runs:
+            for bank_key, raw_key in run:
+                if raw_key not in load_order:
+                    load_order.append(raw_key)
 
         raw_t = {}
         bank_t = {}
-        grp_t = {}
-        cod_t = {}
-        state = {"loaded": 0, "used": 0}
+        grouped_t = {}
+        words_t = {}
+        count = {"loaded": 0, "used": 0}
 
-        def nm(bk):
-            return ("%s_" * len(bk)) % tuple(bk)
+        def label(key):
+            return ("%s_" * len(key)) % tuple(key)
 
         def load_upto(n):
-            while state["loaded"] < min(n, len(load_order)):
-                u = load_order[state["loaded"]]
-                t = rawp.tile([P, 2048], BF16, name="raw_" + nm(u), tag="raw")
-                raw_t[u] = t
-                if u[0] == "x":
-                    src = hidden_states[256 * u[1] : 256 * u[1] + 256, :].rearrange("(b p) k -> p b k", p=P)
-                    dst = t[:].rearrange("p (b k) -> p b k", b=2)
-                elif u[0] == 2:
-                    hh, c = u[1], u[2]
+            while count["loaded"] < min(n, len(load_order)):
+                key = load_order[count["loaded"]]
+                raw = raw_pool.tile([P, 2048], BF16, name="raw_" + label(key), tag="raw")
+                raw_t[key] = raw
+                if key[0] == "x":
+                    src = hidden_states[256 * key[1] : 256 * key[1] + 256, :].rearrange("(b p) k -> p b k", p=P)
+                    dst = raw[:].rearrange("p (b k) -> p b k", b=2)
+                elif key[0] == 2:
+                    hh, c = key[1], key[2]
                     src = w2_q[512 * hh : 512 * hh + 512, 512 * c : 512 * c + 512].rearrange("(b p) f -> p b f", p=P)
-                    dst = t[:].rearrange("p (b f) -> p b f", b=4)
+                    dst = raw[:].rearrange("p (b f) -> p b f", b=4)
                 else:
-                    wq = w1_q if u[0] == 1 else w3_q
-                    r0 = 512 * u[1] + 256 * u[2]
-                    src = wq[r0 : r0 + 256, :].rearrange("(p e) k -> p (e k)", e=2)
-                    dst = t[:]
+                    weight = w1_q if key[0] == 1 else w3_q
+                    row0 = 512 * key[1] + 256 * key[2]
+                    src = weight[row0 : row0 + 256, :].rearrange("(p h) k -> p (h k)", h=2)
+                    dst = raw[:]
                 nc.sync.dma_start(out=dst, in_=src)
-                state["loaded"] += 1
+                count["loaded"] += 1
 
-        def t_run(r):
-            for bk, ru in runs[r]:
-                bank = psum.tile([P, 512], F32, name="T_" + nm(bk), tag="T")
-                bank_t[bk] = bank
-                rf = raw_t[ru][:].bitcast(F32)
+        def raw_done(n):
+            count["used"] += n
+            load_upto(count["used"] + RAW_BUFS)
+
+        def transpose_run(r):
+            for bank_key, raw_key in runs[r]:
+                bank = psum.tile([P, 512], F32, name="T_" + label(bank_key), tag="T")
+                bank_t[bank_key] = bank
+                raw_words = raw_t[raw_key][:].bitcast(F32)
                 for u in range(2):
                     for b in range(2):
-                        if bk[0] == 2:
-                            col = (2 * bk[3] + b) * 256 + 128 * u
+                        if bank_key[0] == 2:
+                            col = (2 * bank_key[3] + b) * 256 + 128 * u
                         else:
-                            col = b * 512 + 256 * bk[3] + 128 * u
+                            col = b * 512 + 256 * bank_key[3] + 128 * u
                         nc.tensor.transpose(
-                            bank[:, (2 * u + b) * P : (2 * u + b + 1) * P], rf[:, col : col + P], ident[:]
+                            bank[:, (2 * u + b) * P : (2 * u + b + 1) * P], raw_words[:, col : col + P], ident[:]
                         )
-            state["used"] += 2
-            load_upto(state["used"] + RAW_BUFS)
+            raw_done(2)
 
-        def s_copies(r):
-            grp = grpp.tile([P, 4096], BF16, name="grp_%d" % r, tag="grp", align_bytes=64)
-            grp_t[r] = grp
-            gf = grp[:].bitcast(F32)
+        def empty_run(r):
+            grouped = grouped_pool.tile([P, 4096], BF16, name="grouped_%d" % r, tag="grouped", align_bytes=64)
+            grouped_t[r] = grouped
+            grouped_words = grouped[:].bitcast(F32)
             for i in range(4):
-                bk, ru = runs[r][i]
                 nc.scalar.copy(
-                    out=gf[:, 512 * i : 512 * (i + 1)].rearrange("p (n u) -> p n u", u=2),
-                    in_=bank_t[bk][:].rearrange("p (u n) -> p n u", u=2),
+                    out=grouped_words[:, 512 * i : 512 * (i + 1)].rearrange("p (n u) -> p n u", u=2),
+                    in_=bank_t[runs[r][i][0]][:].rearrange("p (u n) -> p n u", u=2),
                 )
 
-        def v_scale(r, lo, n):
+        def scale_run(r, first_bank, n_banks):
             kind = runs[r][0][0][0]
             cols = 128 if kind == 2 else 64
-            per = 256 // cols
-            first = (r - 14 if kind == 2 else runs[r][0][0][1]) * 4 * per + lo * per
-            view = grp_t[r][:, 1024 * lo : 1024 * (lo + n)].rearrange("p (j n x) -> p j n x", n=cols, x=4)
-            tab = tabs[kind][:, first : first + n * per, :].unsqueeze(2).to_broadcast([P, n * per, cols, 4])
-            nc.vector.tensor_tensor(out=view, in0=view, in1=tab, op=ALU.mult)
+            per_bank = 256 // cols
+            run_in_table = r - 2 * CHUNKS if kind == 2 else runs[r][0][0][1]
+            first = (4 * run_in_table + first_bank) * per_bank
+            view = grouped_t[r][:, 1024 * first_bank : 1024 * (first_bank + n_banks)].rearrange(
+                "p (j n x) -> p j n x", n=cols, x=4
+            )
+            tab = factor_tab[kind][:, first : first + n_banks * per_bank, :]
+            nc.vector.tensor_tensor(
+                out=view, in0=view, in1=tab.unsqueeze(2).to_broadcast([P, n_banks * per_bank, cols, 4]), op=ALU.mult
+            )
 
-        def v_quant(r, lo, n):
-            if r not in cod_t:
-                cd = codp.tile([P, 1024], U32, name="cod_%d" % r, tag="cod", align_bytes=64)
-                cs = codp.tile([P, 1024], U8, name="cos_%d" % r, tag="cos", align_bytes=64)
-                cod_t[r] = (cd, cs)
-            cd, cs = cod_t[r]
-            sl = slice(256 * lo, 256 * (lo + n))
+        def quantise_run(r, first_bank, n_banks):
+            if r not in words_t:
+                words_new = words_pool.tile([P, 1024], U32, name="words_%d" % r, tag="words", align_bytes=64)
+                scales_new = words_pool.tile([P, 1024], U8, name="scales_%d" % r, tag="scales", align_bytes=64)
+                words_t[r] = (words_new, scales_new)
+            words, scales = words_t[r]
+            cols = slice(256 * first_bank, 256 * (first_bank + n_banks))
             nc.vector.quantize_mx(
-                out=cd[:, sl].bitcast(FP8X4), scales=cs[:, sl], in_=grp_t[r][:, 1024 * lo : 1024 * (lo + n)]
+                out=words[:, cols].bitcast(FP8X4),
+                scales=scales[:, cols],
+                in_=grouped_t[r][:, 1024 * first_bank : 1024 * (first_bank + n_banks)],
             )
 
         load_upto(RAW_BUFS)
-        t_run(0)
-        s_copies(0)
-        v_scale(0, 0, 2)
-        v_scale(0, 2, 2)
-        xgf = xg[:].bitcast(F32).rearrange("p (g t r u) -> p t g r u", g=2, t=4, r=P, u=2)
-        xbanks = []
+        transpose_run(0)
+        empty_run(0)
+        scale_run(0, 0, 2)
+        scale_run(0, 2, 2)
+        x_view = x_grouped[:].bitcast(F32).rearrange("p (g t r u) -> p t g r u", g=2, t=4, r=P, u=2)
+        x_banks = []
         for t in range(4):
             bank = psum.tile([P, 512], F32, name="TX_%d" % t, tag="T")
-            xbanks.append(bank)
-            rf = raw_t[("x", t // 2)][:].bitcast(F32)
+            x_banks.append(bank)
+            raw_words = raw_t[("x", t // 2)][:].bitcast(F32)
             for u in range(2):
                 for g in range(2):
                     col = (t % 2) * 512 + 256 * g + 128 * u
-                    nc.tensor.transpose(bank[:, (2 * u + g) * P : (2 * u + g + 1) * P], rf[:, col : col + P], ident[:])
+                    nc.tensor.transpose(
+                        bank[:, (2 * u + g) * P : (2 * u + g + 1) * P], raw_words[:, col : col + P], ident[:]
+                    )
         for t in range(4):
-            src = xbanks[t][:].rearrange("p (u g r) -> p g r u", u=2, g=2, r=P)
-            nc.scalar.copy(out=xgf[:, t], in_=src)
-        v_quant(0, 0, 2)
-        v_quant(0, 2, 2)
+            nc.scalar.copy(out=x_view[:, t], in_=x_banks[t][:].rearrange("p (u g r) -> p g r u", u=2, g=2, r=P))
+        quantise_run(0, 0, 2)
+        quantise_run(0, 2, 2)
         for g in range(2):
             nc.vector.quantize_mx(
-                out=xc[:, g, :].bitcast(FP8X4), scales=xs[:, g, :], in_=xg[:, 2048 * g : 2048 * (g + 1)]
+                out=x_words[:, g, :].bitcast(FP8X4),
+                scales=x_scales[:, g, :],
+                in_=x_grouped[:, 2048 * g : 2048 * (g + 1)],
             )
-        state["used"] += 2
-        load_upto(state["used"] + RAW_BUFS)
+        raw_done(2)
+        for r in range(1, AHEAD):
+            transpose_run(r)
+            empty_run(r)
+            scale_run(r, 0, 4)
+            quantise_run(r, 0, 4)
 
-        for r in range(1, LA):
-            t_run(r)
-            s_copies(r)
-            v_scale(r, 0, 4)
-            v_quant(r, 0, 4)
+        mx_t = {}
+        silu_t = {}
+        fused_t = {}
 
-        gu_t = {}
-        sg_t = {}
-        fg_t = {}
-
-        def mm1(kind, w, c, tb):
-            bank = psum.tile([P, 512], F32, name="%s_%d_%d" % (kind, c, tb), tag="GU")
-            gu_t[(kind, c, tb)] = bank
-            cd, cs = cod_t[2 * c + (0 if w == 1 else 1)]
-            for tau in range(4):
-                up, e = tau // 2, tau % 2
+        def stage1_bank(kind, c, tb):
+            bank = psum.tile([P, 512], F32, name="%s_%d_%d" % (kind, c, tb), tag="MX")
+            mx_t[(kind, c, tb)] = bank
+            words, scales = words_t[2 * c + (0 if kind == "g" else 1)]
+            for tile4 in range(4):
+                a, h = tile4 // 2, tile4 % 2
                 for g in range(2):
-                    col = ((up * 2 + g) * 2 + e) * P
+                    col = ((a * 2 + g) * 2 + h) * P
                     nc.tensor.matmul_mx(
-                        out=bank[:, tau * P : (tau + 1) * P],
-                        lhsT=cd[:, col : col + P].bitcast(FP8X4),
-                        lhsT_scale=cs[:, col : col + P],
-                        rhs=xc[:, g, tb * P : (tb + 1) * P].bitcast(FP8X4),
-                        rhs_scale=xs[:, g, tb * P : (tb + 1) * P],
+                        out=bank[:, tile4 * P : (tile4 + 1) * P],
+                        lhsT=words[:, col : col + P].bitcast(FP8X4),
+                        lhsT_scale=scales[:, col : col + P],
+                        rhs=x_words[:, g, tb * P : (tb + 1) * P].bitcast(FP8X4),
+                        rhs_scale=x_scales[:, g, tb * P : (tb + 1) * P],
                         start=(g == 0),
                         stop=(g == 1),
                     )
 
-        def s_act(k):
-            c, h = k // 2, k % 2
-            sg = sgp.tile([P, 2, P, 4], F32, name="sg_%d" % k, tag="sg")
-            sg_t[k] = sg
+        def silu_step(k):
+            c, half = k // 2, k % 2
+            act = silu_pool.tile([P, 2, P, 4], F32, name="silu_%d" % k, tag="silu")
+            silu_t[k] = act
             for i in range(2):
-                tb = 2 * h + i
                 nc.scalar.activation(
-                    out=sg[:, i], in_=gu_t[("g", c, tb)][:].rearrange("p (t r) -> p r t", t=4), func=ACT.Silu
+                    out=act[:, i],
+                    in_=mx_t[("g", c, 2 * half + i)][:].rearrange("p (t r) -> p r t", t=4),
+                    func=ACT.Silu,
                 )
 
-        def v_gate(k):
-            c, h = k // 2, k % 2
-            if c not in fg_t:
-                fg_t[c] = fgp.tile([P, 2, 1024], BF16, name="fg_%d" % c, tag="fg", align_bytes=64)
+        def product_step(k):
+            c, half = k // 2, k % 2
+            if c not in fused_t:
+                fused_t[c] = fused_pool.tile([P, 2, 1024], BF16, name="fused_%d" % c, tag="fused", align_bytes=64)
             for i in range(2):
                 nc.vector.tensor_tensor(
-                    out=fg_t[c][:, h, 512 * i : 512 * (i + 1)].rearrange("p (r t) -> p r t", t=4),
-                    in0=gu_t[("u", c, 2 * h + i)][:].rearrange("p (t r) -> p r t", t=4),
-                    in1=sg_t[k][:, i],
+                    out=fused_t[c][:, half, 512 * i : 512 * (i + 1)].rearrange("p (r t) -> p r t", t=4),
+                    in0=mx_t[("u", c, 2 * half + i)][:].rearrange("p (t r) -> p r t", t=4),
+                    in1=silu_t[k][:, i],
                     op=ALU.mult,
                 )
 
-        def v_qf(c):
+        def quantise_fused(c):
             nc.vector.quantize_mx(
-                out=fc[:, c, :].bitcast(FP8X4), scales=fs[:, c, :], in_=fg_t[c][:].rearrange("p a x -> p (a x)")
+                out=f_words[:, c, :].bitcast(FP8X4),
+                scales=f_scales[:, c, :],
+                in_=fused_t[c][:].rearrange("p a x -> p (a x)"),
             )
 
-        acc_t = {}
-        for k in range(21):
-            r = k + LA
-            if r < 21:
-                t_run(r)
-                s_copies(r)
-            if 1 <= k <= 14:
-                v_gate(k - 1)
-            if 13 <= k <= 16:
-                for c in range(2 * (k - 13), min(2 * (k - 13) + 2, 7)):
-                    v_qf(c)
-            if LA < r <= 21:
-                v_quant(r - 1, 0, 4)
-            if r < 21:
-                v_scale(r, 0, 4)
-            if k < 14:
-                c, h = k // 2, k % 2
-                for tb in (2 * h, 2 * h + 1):
-                    mm1("g", 1, c, tb)
-                    mm1("u", 3, c, tb)
-                s_act(k)
+        def stage2_unit(r, i):
+            hh, c = units2[2 * (r - 2 * CHUNKS) + i]
+            words, scales = words_t[r]
+            for tb in range(4):
+                if c == 0:
+                    mx_t[("out", hh, tb)] = psum.tile([P, 512], F32, name="acc_%d_%d" % (hh, tb), tag="MX")
+                acc = mx_t[("out", hh, tb)]
+                nc.tensor.matmul_mx(
+                    out=acc[:],
+                    lhsT=f_words[:, c, tb * P : (tb + 1) * P].bitcast(FP8X4),
+                    lhsT_scale=f_scales[:, c, tb * P : (tb + 1) * P],
+                    rhs=words[:, 512 * i : 512 * (i + 1)].bitcast(FP8X4),
+                    rhs_scale=scales[:, 512 * i : 512 * (i + 1)],
+                    start=(c == 0),
+                    stop=(c == CHUNKS - 1),
+                )
+                if c == CHUNKS - 1:
+                    result = out_pool.tile([P, 512], F32, name="result_%d_%d" % (hh, tb), tag="result")
+                    if tb % 2 == 0 or hh == 0:
+                        nc.scalar.copy(out=result[:], in_=acc[:])
+                    else:
+                        nc.vector.tensor_copy(out=result[:], in_=acc[:])
+                    nc.sync.dma_start(out=out[tb * P : (tb + 1) * P, hh * 512 : (hh + 1) * 512], in_=result[:])
+
+        stage1_steps = 2 * CHUNKS
+        for k in range(n_runs):
+            r = k + AHEAD
+            if r < n_runs:
+                transpose_run(r)
+                empty_run(r)
+            if 1 <= k <= stage1_steps:
+                product_step(k - 1)
+            if stage1_steps - 1 <= k <= stage1_steps + 2:
+                first = 2 * (k - stage1_steps + 1)
+                for c in range(first, min(first + 2, CHUNKS)):
+                    quantise_fused(c)
+            if AHEAD < r <= n_runs:
+                quantise_run(r - 1, 0, 4)
+            if r < n_runs:
+                scale_run(r, 0, 4)
+            if k < stage1_steps:
+                for tb in (2 * (k % 2), 2 * (k % 2) + 1):
+                    stage1_bank("g", k // 2, tb)
+                    stage1_bank("u", k // 2, tb)
+                silu_step(k)
             else:
-                j = k - 14
-                cd, cs = cod_t[k]
-                for i, u2 in enumerate((units2[2 * j], units2[2 * j + 1])):
-                    hh, c = u2
-                    for tb in range(4):
-                        if c == 0:
-                            acc_t[(hh, tb)] = psum.tile([P, 512], F32, name="acc_%d_%d" % (hh, tb), tag="GU")
-                        acc = acc_t[(hh, tb)]
-                        nc.tensor.matmul_mx(
-                            out=acc[:],
-                            lhsT=fc[:, c, tb * P : (tb + 1) * P].bitcast(FP8X4),
-                            lhsT_scale=fs[:, c, tb * P : (tb + 1) * P],
-                            rhs=cd[:, 512 * i : 512 * (i + 1)].bitcast(FP8X4),
-                            rhs_scale=cs[:, 512 * i : 512 * (i + 1)],
-                            start=(c == 0),
-                            stop=(c == 6),
-                        )
-                        if c == 6:
-                            ob = obp.tile([P, 512], F32, name="ob_%d_%d" % (hh, tb), tag="ob")
-                            if tb % 2 == 0 or hh == 0:
-                                nc.scalar.copy(out=ob[:], in_=acc[:])
-                            else:
-                                nc.vector.tensor_copy(out=ob[:], in_=acc[:])
-                            nc.sync.dma_start(
-                                out=out[tb * P : (tb + 1) * P, hh * 512 : (hh + 1) * 512], in_=ob[:]
-                            )
+                for i in range(2):
+                    stage2_unit(k, i)

from contextlib import ExitStack

import concourse.mybir as mybir
from concourse.masks import make_identity

F32 = mybir.dt.float32
BF16 = mybir.dt.bfloat16
U32 = mybir.dt.uint32
U8 = mybir.dt.uint8
FP8X4 = mybir.dt.float8_e4m3fn_x4
ACT = mybir.ActivationFunctionType
ALU = mybir.AluOpType

T, H, F = 512, 1024, 3584
P = 128
CHUNKS = F // 512
FLOPS = 2 * T * H * F * 3

AHEAD = 3
RAW_BUFS = 16


def tile_blocksparsetop2mlphffp8_kernel(tc, hidden_states, w1_q, w1_s, w3_q, w3_s, w2_q, w2_s, out):
    nc = tc.nc
    with ExitStack() as ctx:
        const = ctx.enter_context(tc.tile_pool(name="const", bufs=1))
        raw_pool = ctx.enter_context(tc.tile_pool(name="raw_pool", bufs=RAW_BUFS))
        grouped_pool = ctx.enter_context(tc.tile_pool(name="grouped_pool", bufs=3))
        words_pool = ctx.enter_context(tc.tile_pool(name="words_pool", bufs=AHEAD + 4))
        silu_pool = ctx.enter_context(tc.tile_pool(name="silu_pool", bufs=3))
        fused_pool = ctx.enter_context(tc.tile_pool(name="fused_pool", bufs=CHUNKS))
        out_pool = ctx.enter_context(tc.tile_pool(name="out_pool", bufs=4))
        psum = ctx.enter_context(tc.psum_pool(name="psum", bufs=4))
        ctx.enter_context(tc.manual_schedule())

        factors_row = const.tile([P, 768], BF16, name="factors_row")
        nc.vector.memset(factors_row[:], 0.0)
        for i, table in enumerate((w1_s, w3_s, w2_s)):
            nc.sync.dma_start(
                out=factors_row[0:1, 224 * i : 224 * (i + 1)], in_=table.rearrange("a b -> (a b)").unsqueeze(0)
            )
        ones = const.tile([P, P], BF16, name="ones")
        nc.vector.memset(ones[:], 1.0)
        ident = const.tile([P, P], F32, name="ident")
        make_identity(nc, ident[:])
        warm_in = const.tile([P, 1], F32, name="warm_in")
        warm_out = const.tile([P, 1], F32, name="warm_out")
        nc.vector.memset(warm_in[:], 0.0)
        nc.scalar.activation(out=warm_out[:], in_=warm_in[:], func=ACT.Silu)

        spread_a = psum.tile([P, 512], F32, name="spread_a", tag="T")
        spread_b = psum.tile([P, 512], F32, name="spread_b", tag="T")
        nc.tensor.matmul(out=spread_a[:], lhsT=ones[:], rhs=factors_row[:, 0:512], start=True, stop=True)
        nc.tensor.matmul(out=spread_b[:, 0:256], lhsT=ones[:], rhs=factors_row[:, 512:768], start=True, stop=True)
        pairs = const.tile([P, 336, 2], BF16, name="pairs")
        for half in range(2):
            rows = slice(64 * half, 64 * half + 64)
            nc.vector.tensor_copy(
                out=pairs[rows, 0:256, :],
                in_=spread_a[rows, :]
                .rearrange("p (m h) -> p m h", h=2)[:, :, half : half + 1]
                .to_broadcast([64, 256, 2]),
            )
            nc.vector.tensor_copy(
                out=pairs[rows, 256:336, :],
                in_=spread_b[rows, 0:160]
                .rearrange("p (m h) -> p m h", h=2)[:, :, half : half + 1]
                .to_broadcast([64, 80, 2]),
            )
        factor_tab = {}
        for i, w in enumerate((1, 3)):
            tab = const.tile([P, 112, 4], BF16, name="tab%d" % w)
            factor_tab[w] = tab
            for g in range(2):
                for h in range(2):
                    nc.vector.tensor_copy(
                        out=tab[:].rearrange("p (a g h r) x -> p a g h r x", g=2, h=2, r=2)[:, :, g, h, :, :],
                        in_=pairs[:, 112 * i : 112 * (i + 1), :].rearrange(
                            "p (a r g u) e -> p a r g (u e)", r=2, g=2, u=2
                        )[:, :, :, g, :],
                    )
        tab2 = const.tile([P, 56, 4], BF16, name="tab2")
        factor_tab[2] = tab2
        for hh in range(2):
            nc.vector.tensor_copy(
                out=tab2[:, 28 * hh : 28 * (hh + 1), :].rearrange("p (c b) x -> p c b x", b=4),
                in_=pairs[:, 224:336, :].rearrange("p (hh b c u) e -> p hh c b (u e)", hh=2, b=4, c=7, u=2)[:, hh],
            )

        x_grouped = const.tile([P, 4096], BF16, name="x_grouped", align_bytes=64)
        x_words = const.tile([P, 2, 512], U32, name="x_words", align_bytes=64)
        x_scales = const.tile([P, 2, 512], U8, name="x_scales", align_bytes=64)
        f_words = const.tile([P, CHUNKS, 512], U32, name="f_words", align_bytes=64)
        f_scales = const.tile([P, CHUNKS, 512], U8, name="f_scales", align_bytes=64)

        runs = []
        for c in range(CHUNKS):
            for w in (1, 3):
                runs.append([((w, c, a, g), (w, c, a)) for a in range(2) for g in range(2)])
        units2 = [(hh, c) for hh in range(2) for c in range(CHUNKS)]
        for j in range(CHUNKS):
            runs.append([((2,) + u + (q,), (2,) + u) for u in (units2[2 * j], units2[2 * j + 1]) for q in range(2)])
        n_runs = len(runs)
        load_order = [(1, 0, 0), (1, 0, 1), ("x", 0), ("x", 1)]
        for run in runs:
            for bank_key, raw_key in run:
                if raw_key not in load_order:
                    load_order.append(raw_key)

        raw_t = {}
        bank_t = {}
        grouped_t = {}
        words_t = {}
        count = {"loaded": 0, "used": 0}

        def label(key):
            return ("%s_" * len(key)) % tuple(key)

        def load_upto(n):
            while count["loaded"] < min(n, len(load_order)):
                key = load_order[count["loaded"]]
                raw = raw_pool.tile([P, 2048], BF16, name="raw_" + label(key), tag="raw")
                raw_t[key] = raw
                if key[0] == "x":
                    src = hidden_states[256 * key[1] : 256 * key[1] + 256, :].rearrange("(b p) k -> p b k", p=P)
                    dst = raw[:].rearrange("p (b k) -> p b k", b=2)
                elif key[0] == 2:
                    hh, c = key[1], key[2]
                    src = w2_q[512 * hh : 512 * hh + 512, 512 * c : 512 * c + 512].rearrange("(b p) f -> p b f", p=P)
                    dst = raw[:].rearrange("p (b f) -> p b f", b=4)
                else:
                    weight = w1_q if key[0] == 1 else w3_q
                    row0 = 512 * key[1] + 256 * key[2]
                    src = weight[row0 : row0 + 256, :].rearrange("(p h) k -> p (h k)", h=2)
                    dst = raw[:]
                nc.sync.dma_start(out=dst, in_=src)
                count["loaded"] += 1

        def raw_done(n):
            count["used"] += n
            load_upto(count["used"] + RAW_BUFS)

        def transpose_run(r):
            for bank_key, raw_key in runs[r]:
                bank = psum.tile([P, 512], F32, name="T_" + label(bank_key), tag="T")
                bank_t[bank_key] = bank
                raw_words = raw_t[raw_key][:].bitcast(F32)
                for u in range(2):
                    for b in range(2):
                        if bank_key[0] == 2:
                            col = (2 * bank_key[3] + b) * 256 + 128 * u
                        else:
                            col = b * 512 + 256 * bank_key[3] + 128 * u
                        nc.tensor.transpose(
                            bank[:, (2 * u + b) * P : (2 * u + b + 1) * P], raw_words[:, col : col + P], ident[:]
                        )
            raw_done(2)

        def empty_run(r):
            grouped = grouped_pool.tile([P, 4096], BF16, name="grouped_%d" % r, tag="grouped", align_bytes=64)
            grouped_t[r] = grouped
            grouped_words = grouped[:].bitcast(F32)
            for i in range(4):
                nc.scalar.copy(
                    out=grouped_words[:, 512 * i : 512 * (i + 1)].rearrange("p (n u) -> p n u", u=2),
                    in_=bank_t[runs[r][i][0]][:].rearrange("p (u n) -> p n u", u=2),
                )

        def scale_run(r, first_bank, n_banks):
            kind = runs[r][0][0][0]
            cols = 128 if kind == 2 else 64
            per_bank = 256 // cols
            run_in_table = r - 2 * CHUNKS if kind == 2 else runs[r][0][0][1]
            first = (4 * run_in_table + first_bank) * per_bank
            view = grouped_t[r][:, 1024 * first_bank : 1024 * (first_bank + n_banks)].rearrange(
                "p (j n x) -> p j n x", n=cols, x=4
            )
            tab = factor_tab[kind][:, first : first + n_banks * per_bank, :]
            nc.vector.tensor_tensor(
                out=view, in0=view, in1=tab.unsqueeze(2).to_broadcast([P, n_banks * per_bank, cols, 4]), op=ALU.mult
            )

        def quantise_run(r, first_bank, n_banks):
            if r not in words_t:
                words_new = words_pool.tile([P, 1024], U32, name="words_%d" % r, tag="words", align_bytes=64)
                scales_new = words_pool.tile([P, 1024], U8, name="scales_%d" % r, tag="scales", align_bytes=64)
                words_t[r] = (words_new, scales_new)
            words, scales = words_t[r]
            cols = slice(256 * first_bank, 256 * (first_bank + n_banks))
            nc.vector.quantize_mx(
                out=words[:, cols].bitcast(FP8X4),
                scales=scales[:, cols],
                in_=grouped_t[r][:, 1024 * first_bank : 1024 * (first_bank + n_banks)],
            )

        load_upto(RAW_BUFS)
        transpose_run(0)
        empty_run(0)
        scale_run(0, 0, 2)
        scale_run(0, 2, 2)
        x_view = x_grouped[:].bitcast(F32).rearrange("p (g t r u) -> p t g r u", g=2, t=4, r=P, u=2)
        x_banks = []
        for t in range(4):
            bank = psum.tile([P, 512], F32, name="TX_%d" % t, tag="T")
            x_banks.append(bank)
            raw_words = raw_t[("x", t // 2)][:].bitcast(F32)
            for u in range(2):
                for g in range(2):
                    col = (t % 2) * 512 + 256 * g + 128 * u
                    nc.tensor.transpose(
                        bank[:, (2 * u + g) * P : (2 * u + g + 1) * P], raw_words[:, col : col + P], ident[:]
                    )
        for t in range(4):
            nc.scalar.copy(out=x_view[:, t], in_=x_banks[t][:].rearrange("p (u g r) -> p g r u", u=2, g=2, r=P))
        quantise_run(0, 0, 2)
        quantise_run(0, 2, 2)
        for g in range(2):
            nc.vector.quantize_mx(
                out=x_words[:, g, :].bitcast(FP8X4),
                scales=x_scales[:, g, :],
                in_=x_grouped[:, 2048 * g : 2048 * (g + 1)],
            )
        raw_done(2)
        for r in range(1, AHEAD):
            transpose_run(r)
            empty_run(r)
            scale_run(r, 0, 4)
            quantise_run(r, 0, 4)

        mx_t = {}
        silu_t = {}
        fused_t = {}

        def stage1_bank(kind, c, tb):
            bank = psum.tile([P, 512], F32, name="%s_%d_%d" % (kind, c, tb), tag="MX")
            mx_t[(kind, c, tb)] = bank
            words, scales = words_t[2 * c + (0 if kind == "g" else 1)]
            for tile4 in range(4):
                a, h = tile4 // 2, tile4 % 2
                for g in range(2):
                    col = ((a * 2 + g) * 2 + h) * P
                    nc.tensor.matmul_mx(
                        out=bank[:, tile4 * P : (tile4 + 1) * P],
                        lhsT=words[:, col : col + P].bitcast(FP8X4),
                        lhsT_scale=scales[:, col : col + P],
                        rhs=x_words[:, g, tb * P : (tb + 1) * P].bitcast(FP8X4),
                        rhs_scale=x_scales[:, g, tb * P : (tb + 1) * P],
                        start=(g == 0),
                        stop=(g == 1),
                    )

        def silu_step(k):
            c, half = k // 2, k % 2
            act = silu_pool.tile([P, 2, P, 4], F32, name="silu_%d" % k, tag="silu")
            silu_t[k] = act
            for i in range(2):
                nc.scalar.activation(
                    out=act[:, i],
                    in_=mx_t[("g", c, 2 * half + i)][:].rearrange("p (t r) -> p r t", t=4),
                    func=ACT.Silu,
                )

        def product_step(k):
            c, half = k // 2, k % 2
            if c not in fused_t:
                fused_t[c] = fused_pool.tile([P, 2, 1024], BF16, name="fused_%d" % c, tag="fused", align_bytes=64)
            for i in range(2):
                nc.vector.tensor_tensor(
                    out=fused_t[c][:, half, 512 * i : 512 * (i + 1)].rearrange("p (r t) -> p r t", t=4),
                    in0=mx_t[("u", c, 2 * half + i)][:].rearrange("p (t r) -> p r t", t=4),
                    in1=silu_t[k][:, i],
                    op=ALU.mult,
                )

        def quantise_fused(c):
            nc.vector.quantize_mx(
                out=f_words[:, c, :].bitcast(FP8X4),
                scales=f_scales[:, c, :],
                in_=fused_t[c][:].rearrange("p a x -> p (a x)"),
            )

        def stage2_unit(r, i):
            hh, c = units2[2 * (r - 2 * CHUNKS) + i]
            words, scales = words_t[r]
            for tb in range(4):
                if c == 0:
                    mx_t[("out", hh, tb)] = psum.tile([P, 512], F32, name="acc_%d_%d" % (hh, tb), tag="MX")
                acc = mx_t[("out", hh, tb)]
                nc.tensor.matmul_mx(
                    out=acc[:],
                    lhsT=f_words[:, c, tb * P : (tb + 1) * P].bitcast(FP8X4),
                    lhsT_scale=f_scales[:, c, tb * P : (tb + 1) * P],
                    rhs=words[:, 512 * i : 512 * (i + 1)].bitcast(FP8X4),
                    rhs_scale=scales[:, 512 * i : 512 * (i + 1)],
                    start=(c == 0),
                    stop=(c == CHUNKS - 1),
                )
                if c == CHUNKS - 1:
                    result = out_pool.tile([P, 512], F32, name="result_%d_%d" % (hh, tb), tag="result")
                    if tb % 2 == 0 or hh == 0:
                        nc.scalar.copy(out=result[:], in_=acc[:])
                    else:
                        nc.vector.tensor_copy(out=result[:], in_=acc[:])
                    nc.sync.dma_start(out=out[tb * P : (tb + 1) * P, hh * 512 : (hh + 1) * 512], in_=result[:])

        stage1_steps = 2 * CHUNKS
        for k in range(n_runs):
            r = k + AHEAD
            if r < n_runs:
                transpose_run(r)
                empty_run(r)
            if 1 <= k <= stage1_steps:
                product_step(k - 1)
            if stage1_steps - 1 <= k <= stage1_steps + 2:
                first = 2 * (k - stage1_steps + 1)
                for c in range(first, min(first + 2, CHUNKS)):
                    quantise_fused(c)
            if AHEAD < r <= n_runs:
                quantise_run(r - 1, 0, 4)
            if r < n_runs:
                scale_run(r, 0, 4)
            if k < stage1_steps:
                for tb in (2 * (k % 2), 2 * (k % 2) + 1):
                    stage1_bank("g", k // 2, tb)
                    stage1_bank("u", k // 2, tb)
                silu_step(k)
            else:
                for i in range(2):
                    stage2_unit(k, i)
